import numpy as np
import ml_dtypes

BF16 = ml_dtypes.bfloat16


def bf(x):
    return np.asarray(x, np.float32).astype(BF16)


def f32(x):
    return np.asarray(x, np.float32)


def f64(x):
    return np.asarray(x).astype(np.float64)


def striped(idx):
    return np.tile(idx.reshape(-1, 16).T, (8, 1))


V, D, H1, H2, NC, T, B, N = 512, 128, 512, 4096, 512, 4, 256, 1024
QS = 0.5
EPS = 1e-5
A1, A2, A3 = 0.5, 0.25, 0.0625


def erf(a):
    c = np.clip(a, -6.0, 6.0)
    term = c.copy()
    total = c.copy()
    for n in range(1, 150):
        term = term * 2.0 * c * c / (2 * n + 1)
        total = total + term
    r = 2.0 / np.sqrt(np.pi) * np.exp(-c * c) * total
    return np.where(np.abs(a) > 6.0, np.sign(a), r)


def gelu_erf(v):
    return 0.5 * v * (1.0 + erf(v / np.sqrt(2.0)))


def layer_norm(y, gain, shift):
    mu = y.mean(axis=0, keepdims=True)
    var = np.square(y - mu).mean(axis=0, keepdims=True)
    return (y - mu) / np.sqrt(var + EPS) * gain + shift


def ternary(rows, cols, a):
    n = rows * cols
    v = np.concatenate([np.zeros(n // 2), np.full(n // 4, a), np.full(n // 4, -a)])
    return bf(np.random.permutation(v).reshape(rows, cols))


def setup_inputs():
    return {"table": bf(np.random.standard_normal((V, D))), "w1": ternary(D, H1, A1), "b1": f32(0.1 * np.random.standard_normal((H1, 1))), "gain1": f32(1.0 + 0.1 * np.random.standard_normal((H1, 1))), "shift1": f32(0.1 * np.random.standard_normal((H1, 1))), "w2": ternary(H1, H2, A2), "b2": f32(0.1 * np.random.standard_normal((H2, 1))), "gain2": f32(1.0 + 0.1 * np.random.standard_normal((H2, 1))), "shift2": f32(0.1 * np.random.standard_normal((H2, 1))), "w3": ternary(H2, NC, A3), "b3": f32(0.1 * np.random.standard_normal((NC, 1))), "offs": striped(np.random.permutation(np.tile(np.arange(V), 2))[:N])}


def reference(table, w1, b1, gain1, shift1, w2, b2, gain2, shift2, w3, b3, offs):
    idx = offs[:16].T.reshape(-1)
    p = f64(w1).T @ f64(table)[idx].T
    y1 = QS * p.reshape(H1, T, B).sum(axis=1) / T + f64(b1)
    h1 = gelu_erf(layer_norm(y1, f64(gain1), f64(shift1)))
    y2 = QS * (f64(w2).T @ h1) + f64(b2)
    h2 = gelu_erf(layer_norm(y2, f64(gain2), f64(shift2)))
    return QS * (f64(w3).T @ h2) + f64(b3)

@@ -1,0 +1,167 @@
+import concourse.mybir as mybir
+from concourse.masks import make_identity
+
+BF16, F32, U16 = mybir.dt.bfloat16, mybir.dt.float32, mybir.dt.uint16
+ACT = mybir.ActivationFunctionType
+ALU = mybir.AluOpType
+
+P = 128
+V, D, H1, H2, NC = 512, 128, 512, 4096, 512
+T, B = 4, 256
+N = T * B
+QS = 0.5
+EPS = 1e-5
+
+H1_BLOCKS, H2_BLOCKS, NC_BLOCKS = H1 // P, H2 // P, NC // P
+W2_CHUNKS = 4
+W2_CHUNK_BLOCKS = H2_BLOCKS // W2_CHUNKS
+W3_CHUNKS = 8
+W3_CHUNK_BLOCKS = H2_BLOCKS // W3_CHUNKS
+
+ROW_B2, ROW_GAIN2, ROW_SHIFT2 = 0, H2_BLOCKS, 2 * H2_BLOCKS
+ROW_B1 = 3 * H2_BLOCKS
+ROW_GAIN1, ROW_SHIFT1, ROW_B3 = ROW_B1 + H1_BLOCKS, ROW_B1 + 2 * H1_BLOCKS, ROW_B1 + 3 * H1_BLOCKS
+
+FLOPS = 2 * (D * H1 * N + H1 * H2 * B + H2 * NC * B)
+
+
+def tile_ternarycreditrisknet_b_kernel(
+    tc, table, w1, b1, gain1, shift1, w2, b2, gain2, shift2, w3, b3, offs, out
+):
+    nc = tc.nc
+    with (
+        tc.tile_pool(name="held", bufs=1) as held,
+        tc.tile_pool(name="work", bufs=3) as work,
+        tc.psum_pool(name="setup_ps", bufs=1) as setup_ps,
+        tc.psum_pool(name="stats_ps", bufs=1) as stats_ps,
+        tc.psum_pool(name="prod_ps", bufs=4) as prod_ps,
+    ):
+        offsets = held.tile([P, N // 16], U16, name="offsets")
+        nc.sync.dma_start(offsets[:], offs)
+        table_rows = held.tile([P, V // P, D], BF16, name="table_rows")
+        nc.sync.dma_start(table_rows[:], table.rearrange("(a p) d -> p a d", p=P))
+        w1_sb = held.tile([D, H1], BF16, name="w1_sb")
+        nc.scalar.dma_start(w1_sb[:], w1)
+
+        vector_rows = held.tile([P, P], F32, name="vector_rows")
+        nc.vector.memset(vector_rows[:], 0.0)
+        for vector, row in (
+            (b1, ROW_B1), (gain1, ROW_GAIN1), (shift1, ROW_SHIFT1),
+            (b2, ROW_B2), (gain2, ROW_GAIN2), (shift2, ROW_SHIFT2), (b3, ROW_B3),
+        ):
+            blocks = vector.shape[0] // P
+            nc.scalar.dma_start(
+                vector_rows[row : row + blocks, :], vector.rearrange("(a p) o -> a (p o)", p=P)
+            )
+
+        w2_view = w2.rearrange("(k p) u -> p k u", p=P)
+        w2_chunks = []
+        for c in range(W2_CHUNKS):
+            chunk = held.tile([P, H1_BLOCKS, H2 // W2_CHUNKS], BF16, name=f"w2_chunk{c}")
+            nc.sync.dma_start(chunk[:], w2_view[:, :, c * (H2 // W2_CHUNKS) : (c + 1) * (H2 // W2_CHUNKS)])
+            w2_chunks.append(chunk)
+        w3_view = w3.rearrange("(a p) q -> p a q", p=P)
+        w3_chunks = []
+        for c in range(W3_CHUNKS):
+            chunk = held.tile([P, W3_CHUNK_BLOCKS, NC], BF16, name=f"w3_chunk{c}")
+            nc.sync.dma_start(chunk[:], w3_view[:, c * W3_CHUNK_BLOCKS : (c + 1) * W3_CHUNK_BLOCKS, :])
+            w3_chunks.append(chunk)
+
+        identity_bf16 = held.tile([P, P], BF16, name="identity_bf16")
+        make_identity(nc, identity_bf16[:])
+        identity_f32 = held.tile([P, P], F32, name="identity_f32")
+        make_identity(nc, identity_f32[:])
+        mean_of_h1 = held.tile([P, P], F32, name="mean_of_h1")
+        nc.vector.memset(mean_of_h1[:], 1.0 / H1)
+        mean_of_h2 = held.tile([P, P], F32, name="mean_of_h2")
+        nc.vector.memset(mean_of_h2[:], 1.0 / H2)
+
+        table_ps = setup_ps.tile([D, V], BF16, name="table_ps")
+        for a in range(V // P):
+            nc.tensor.transpose(table_ps[:, a * P : (a + 1) * P], table_rows[:, a, :], identity_bf16[:])
+        window = held.tile([D, V], BF16, name="window")
+        nc.vector.tensor_copy(window[:], table_ps[:])
+
+        vector_ps = setup_ps.tile([P, P], F32, name="vector_ps")
+        nc.tensor.transpose(vector_ps[:], vector_rows[:], identity_f32[:])
+        per_feature = held.tile([P, P], F32, name="per_feature")
+        nc.vector.tensor_copy(per_feature[:], vector_ps[:])
+
+        def column(row):
+            return per_feature[:, row : row + 1]
+
+        def leave_psum(prod, scale, bias, y_and_square, sums):
+            nc.scalar.activation(y_and_square[:, 0:B], prod[:], ACT.Identity, bias=bias, scale=scale)
+            nc.scalar.activation(y_and_square[:, B : 2 * B], prod[:], ACT.Square, bias=bias, scale=scale)
+            nc.vector.tensor_tensor(sums[:], sums[:], y_and_square[:], ALU.add)
+
+        def statistics(sums, mean_weights):
+            means = stats_ps.tile([P, 2 * B], F32, name="means")
+            nc.tensor.matmul(means[:], mean_weights[:], sums[:], start=True, stop=True)
+            square_of_mean = work.tile([P, B], F32, name="square_of_mean")
+            nc.scalar.activation(square_of_mean[:], means[:, 0:B], ACT.Square)
+            var = work.tile([P, B], F32, name="var")
+            nc.vector.tensor_tensor(var[:], means[:, B : 2 * B], square_of_mean[:], ALU.subtract)
+            nc.vector.tensor_scalar(var[:], var[:], 0.0, EPS, op0=ALU.max, op1=ALU.add)
+            std = work.tile([P, B], F32, name="std")
+            nc.scalar.activation(std[:], var[:], ACT.Sqrt)
+            rstd = work.tile([P, B], F32, name="rstd")
+            nc.vector.reciprocal(rstd[:], std[:])
+            return means[:, 0:B], rstd
+
+        def norm_gelu(h, y, mean, rstd, gain, shift):
+            normed = work.tile([P, B], F32, name="normed")
+            nc.vector.tensor_tensor(normed[:], y, mean, ALU.subtract)
+            nc.vector.tensor_tensor(normed[:], normed[:], rstd[:], ALU.mult)
+            nc.scalar.activation(h[:], normed[:], ACT.Gelu, bias=shift, scale=gain)
+
+        sums1 = held.tile([P, 2 * B], F32, name="sums1")
+        nc.vector.memset(sums1[:], 0.0)
+        y1 = []
+        for a in range(H1_BLOCKS):
+            prod = prod_ps.tile([P, B], F32, name="prod")
+            for t in range(T):
+                nc.tensor.matmul(
+                    prod[:],
+                    w1_sb[:, a * P : (a + 1) * P],
+                    window[:].indirect(offsets[:, t * (B // 16) : (t + 1) * (B // 16)]),
+                    start=(t == 0),
+                    stop=(t == T - 1),
+                )
+            y1.append(held.tile([P, 2 * B], F32, name=f"y1_{a}"))
+            leave_psum(prod, QS / T, column(ROW_B1 + a), y1[a], sums1)
+        mean1, rstd1 = statistics(sums1, mean_of_h1)
+        h1 = []
+        for a in range(H1_BLOCKS):
+            h1.append(held.tile([P, B], BF16, name=f"h1_{a}"))
+            norm_gelu(h1[a], y1[a][:, 0:B], mean1, rstd1, column(ROW_GAIN1 + a), column(ROW_SHIFT1 + a))
+
+        sums2 = held.tile([P, 2 * B], F32, name="sums2")
+        nc.vector.memset(sums2[:], 0.0)
+        y2 = []
+        for a in range(H2_BLOCKS):
+            chunk, j = w2_chunks[a // W2_CHUNK_BLOCKS], a % W2_CHUNK_BLOCKS
+            prod = prod_ps.tile([P, B], F32, name="prod")
+            for k in range(H1_BLOCKS):
+                nc.tensor.matmul(
+                    prod[:], chunk[:, k, j * P : (j + 1) * P], h1[k][:],
+                    start=(k == 0), stop=(k == H1_BLOCKS - 1),
+                )
+            y2.append(held.tile([P, 2 * B], F32, name=f"y2_{a}"))
+            leave_psum(prod, QS, column(ROW_B2 + a), y2[a], sums2)
+        mean2, rstd2 = statistics(sums2, mean_of_h2)
+
+        out_ps = [prod_ps.tile([P, B], F32, name=f"out_ps{q}", tag="prod") for q in range(NC_BLOCKS)]
+        for a in range(H2_BLOCKS):
+            h2 = work.tile([P, B], BF16, name="h2")
+            norm_gelu(h2, y2[a][:, 0:B], mean2, rstd2, column(ROW_GAIN2 + a), column(ROW_SHIFT2 + a))
+            chunk, j = w3_chunks[a // W3_CHUNK_BLOCKS], a % W3_CHUNK_BLOCKS
+            for q in range(NC_BLOCKS):
+                nc.tensor.matmul(
+                    out_ps[q][:], chunk[:, j, q * P : (q + 1) * P], h2[:],
+                    start=(a == 0), stop=(a == H2_BLOCKS - 1),
+                )
+        for q in range(NC_BLOCKS):
+            out_sb = work.tile([P, B], F32, name="out_sb")
+            nc.scalar.activation(out_sb[:], out_ps[q][:], ACT.Identity, bias=column(ROW_B3 + q), scale=QS)
+            nc.sync.dma_start(out[q * P : (q + 1) * P, :], out_sb[:])

@@ -22,6 +22,8 @@ ROW_B2, ROW_GAIN2, ROW_SHIFT2 = 0, H2_BLOCKS, 2 * H2_BLOCKS
 ROW_B1 = 3 * H2_BLOCKS
 ROW_GAIN1, ROW_SHIFT1, ROW_B3 = ROW_B1 + H1_BLOCKS, ROW_B1 + 2 * H1_BLOCKS, ROW_B1 + 3 * H1_BLOCKS
 
+LEAD = 2
+
 FLOPS = 2 * (D * H1 * N + H1 * H2 * B + H2 * NC * B)
 
 
@@ -31,7 +33,7 @@ def tile_ternarycreditrisknet_b_kernel(
     nc = tc.nc
     with (
         tc.tile_pool(name="held", bufs=1) as held,
-        tc.tile_pool(name="work", bufs=3) as work,
+        tc.tile_pool(name="work", bufs=4) as work,
         tc.psum_pool(name="setup_ps", bufs=1) as setup_ps,
         tc.psum_pool(name="stats_ps", bufs=1) as stats_ps,
         tc.psum_pool(name="prod_ps", bufs=4) as prod_ps,
@@ -90,33 +92,64 @@ def tile_ternarycreditrisknet_b_kernel(
         def column(row):
             return per_feature[:, row : row + 1]
 
-        def leave_psum(prod, scale, bias, y_and_square, sums):
-            nc.scalar.activation(y_and_square[:, 0:B], prod[:], ACT.Identity, bias=bias, scale=scale)
-            nc.scalar.activation(y_and_square[:, B : 2 * B], prod[:], ACT.Square, bias=bias, scale=scale)
-            nc.vector.tensor_tensor(sums[:], sums[:], y_and_square[:], ALU.add)
+        def leave_psum(prod, scale, bias, y, sum_y, sum_sq):
+            nc.scalar.activation(y, prod[:], ACT.Identity, bias=bias, scale=scale)
+            square = work.tile([P, B], F32, name="square")
+            nc.scalar.activation(square[:], prod[:], ACT.Square, bias=bias, scale=scale)
+            nc.vector.tensor_tensor(sum_y[:], sum_y[:], y, ALU.add)
+            nc.vector.tensor_tensor(sum_sq[:], sum_sq[:], square[:], ALU.add)
 
-        def statistics(sums, mean_weights):
-            means = stats_ps.tile([P, 2 * B], F32, name="means")
-            nc.tensor.matmul(means[:], mean_weights[:], sums[:], start=True, stop=True)
+        def statistics(sum_y, sum_sq, mean_weights, layer):
+            mean = stats_ps.tile([P, B], F32, name="mean")
+            nc.tensor.matmul(mean[:], mean_weights[:], sum_y[:], start=True, stop=True)
+            mean_sq = stats_ps.tile([P, B], F32, name="mean_sq")
+            nc.tensor.matmul(mean_sq[:], mean_weights[:], sum_sq[:], start=True, stop=True)
             square_of_mean = work.tile([P, B], F32, name="square_of_mean")
-            nc.scalar.activation(square_of_mean[:], means[:, 0:B], ACT.Square)
-            var = work.tile([P, B], F32, name="var")
-            nc.vector.tensor_tensor(var[:], means[:, B : 2 * B], square_of_mean[:], ALU.subtract)
-            nc.vector.tensor_scalar(var[:], var[:], 0.0, EPS, op0=ALU.max, op1=ALU.add)
-            std = work.tile([P, B], F32, name="std")
-            nc.scalar.activation(std[:], var[:], ACT.Sqrt)
-            rstd = work.tile([P, B], F32, name="rstd")
-            nc.vector.reciprocal(rstd[:], std[:])
-            return means[:, 0:B], rstd
+            nc.scalar.activation(square_of_mean[:], mean[:], ACT.Square)
+            var_eps = work.tile([P, B], F32, name="var_eps")
+            nc.vector.scalar_tensor_tensor(
+                var_eps[:], mean_sq[:], EPS, square_of_mean[:], op0=ALU.add, op1=ALU.subtract
+            )
+            rstd = held.tile([P, B], F32, name=f"rstd{layer}")
+            nc.scalar.activation(rstd[:], var_eps[:], ACT.Abs_reciprocal_sqrt)
+            return mean, rstd
 
-        def norm_gelu(h, y, mean, rstd, gain, shift):
-            normed = work.tile([P, B], F32, name="normed")
-            nc.vector.tensor_tensor(normed[:], y, mean, ALU.subtract)
-            nc.vector.tensor_tensor(normed[:], normed[:], rstd[:], ALU.mult)
-            nc.scalar.activation(h[:], normed[:], ACT.Gelu, bias=shift, scale=gain)
+        def norm_gelu(y, mean, rstd, gain_row, shift_row, new_h, use_h):
+            mean_twice = mean[:].unsqueeze(1).to_broadcast([P, 2, B])
+            rstd_twice = rstd[:].unsqueeze(1).to_broadcast([P, 2, B])
+            centred = []
 
-        sums1 = held.tile([P, 2 * B], F32, name="sums1")
-        nc.vector.memset(sums1[:], 0.0)
+            def centre(g):
+                centred.append(work.tile([P, 2, B], F32, name="centred"))
+                nc.vector.tensor_tensor(centred[g][:], y[g][:], mean_twice, ALU.subtract)
+
+            for g in range(LEAD):
+                centre(g)
+            for g in range(len(y)):
+                if g + LEAD < len(y):
+                    centre(g + LEAD)
+                nc.vector.tensor_tensor(centred[g][:], centred[g][:], rstd_twice, ALU.mult)
+                for i in range(2):
+                    a = 2 * g + i
+                    h = new_h(a)
+                    nc.scalar.activation(
+                        h[:], centred[g][:, i, :], ACT.Gelu,
+                        bias=column(shift_row + a), scale=column(gain_row + a),
+                    )
+                    use_h(a, h)
+
+        def load_rsqrt_table(after):
+            unused = work.tile([P, 1], F32, name="unused")
+            nc.scalar.activation(unused[:], after, ACT.Abs_reciprocal_sqrt, bias=1.0, scale=0.0)
+
+        sum_y1 = held.tile([P, B], F32, name="sum_y1")
+        sum_sq1 = held.tile([P, B], F32, name="sum_sq1")
+        sum_y2 = held.tile([P, B], F32, name="sum_y2")
+        sum_sq2 = held.tile([P, B], F32, name="sum_sq2")
+        for sums in (sum_y1, sum_sq1, sum_y2, sum_sq2):
+            nc.vector.memset(sums[:], 0.0)
+
+        load_rsqrt_table(after=sum_y1[:, 0:1])
         y1 = []
         for a in range(H1_BLOCKS):
             prod = prod_ps.tile([P, B], F32, name="prod")
@@ -128,16 +161,17 @@ def tile_ternarycreditrisknet_b_kernel(
                     start=(t == 0),
                     stop=(t == T - 1),
                 )
-            y1.append(held.tile([P, 2 * B], F32, name=f"y1_{a}"))
-            leave_psum(prod, QS / T, column(ROW_B1 + a), y1[a], sums1)
-        mean1, rstd1 = statistics(sums1, mean_of_h1)
+            if a % 2 == 0:
+                y1.append(held.tile([P, 2, B], F32, name=f"y1_{a // 2}"))
+            leave_psum(prod, QS / T, column(ROW_B1 + a), y1[a // 2][:, a % 2, :], sum_y1, sum_sq1)
+        mean1, rstd1 = statistics(sum_y1, sum_sq1, mean_of_h1, 1)
         h1 = []
-        for a in range(H1_BLOCKS):
-            h1.append(held.tile([P, B], BF16, name=f"h1_{a}"))
-            norm_gelu(h1[a], y1[a][:, 0:B], mean1, rstd1, column(ROW_GAIN1 + a), column(ROW_SHIFT1 + a))
+        norm_gelu(
+            y1, mean1, rstd1, ROW_GAIN1, ROW_SHIFT1,
+            new_h=lambda a: held.tile([P, B], BF16, name=f"h1_{a}"),
+            use_h=lambda a, h: h1.append(h),
+        )
 
-        sums2 = held.tile([P, 2 * B], F32, name="sums2")
-        nc.vector.memset(sums2[:], 0.0)
         y2 = []
         for a in range(H2_BLOCKS):
             chunk, j = w2_chunks[a // W2_CHUNK_BLOCKS], a % W2_CHUNK_BLOCKS
@@ -147,21 +181,33 @@ def tile_ternarycreditrisknet_b_kernel(
                     prod[:], chunk[:, k, j * P : (j + 1) * P], h1[k][:],
                     start=(k == 0), stop=(k == H1_BLOCKS - 1),
                 )
-            y2.append(held.tile([P, 2 * B], F32, name=f"y2_{a}"))
-            leave_psum(prod, QS, column(ROW_B2 + a), y2[a], sums2)
-        mean2, rstd2 = statistics(sums2, mean_of_h2)
+            if a % 2 == 0:
+                y2.append(held.tile([P, 2, B], F32, name=f"y2_{a // 2}"))
+            leave_psum(prod, QS, column(ROW_B2 + a), y2[a // 2][:, a % 2, :], sum_y2, sum_sq2)
+        load_rsqrt_table(after=y2[H2_BLOCKS // 2 - 1][:, 1, 0:1])
+        mean2, rstd2 = statistics(sum_y2, sum_sq2, mean_of_h2, 2)
 
         out_ps = [prod_ps.tile([P, B], F32, name=f"out_ps{q}", tag="prod") for q in range(NC_BLOCKS)]
-        for a in range(H2_BLOCKS):
-            h2 = work.tile([P, B], BF16, name="h2")
-            norm_gelu(h2, y2[a][:, 0:B], mean2, rstd2, column(ROW_GAIN2 + a), column(ROW_SHIFT2 + a))
+
+        def layer3(a, h2):
             chunk, j = w3_chunks[a // W3_CHUNK_BLOCKS], a % W3_CHUNK_BLOCKS
             for q in range(NC_BLOCKS):
                 nc.tensor.matmul(
                     out_ps[q][:], chunk[:, j, q * P : (q + 1) * P], h2[:],
                     start=(a == 0), stop=(a == H2_BLOCKS - 1),
                 )
+
+        norm_gelu(
+            y2, mean2, rstd2, ROW_GAIN2, ROW_SHIFT2,
+            new_h=lambda a: work.tile([P, B], BF16, name="h2"),
+            use_h=layer3,
+        )
+
         for q in range(NC_BLOCKS):
             out_sb = work.tile([P, B], F32, name="out_sb")
-            nc.scalar.activation(out_sb[:], out_ps[q][:], ACT.Identity, bias=column(ROW_B3 + q), scale=QS)
-            nc.sync.dma_start(out[q * P : (q + 1) * P, :], out_sb[:])
+            if q % 2 == 0:
+                nc.scalar.activation(out_sb[:], out_ps[q][:], ACT.Identity, bias=column(ROW_B3 + q), scale=QS)
+                nc.sync.dma_start(out[q * P : (q + 1) * P, :], out_sb[:])
+            else:
+                nc.vector.tensor_scalar(out_sb[:], out_ps[q][:], QS, column(ROW_B3 + q), op0=ALU.mult, op1=ALU.add)
+                nc.scalar.dma_start(out[q * P : (q + 1) * P, :], out_sb[:])

@@ -4,6 +4,7 @@ from concourse.masks import make_identity
 BF16, F32, U16 = mybir.dt.bfloat16, mybir.dt.float32, mybir.dt.uint16
 ACT = mybir.ActivationFunctionType
 ALU = mybir.AluOpType
+ALONG_FREE = mybir.AxisListType.X
 
 P = 128
 V, D, H1, H2, NC = 512, 128, 512, 4096, 512
@@ -13,16 +14,16 @@ QS = 0.5
 EPS = 1e-5
 
 H1_BLOCKS, H2_BLOCKS, NC_BLOCKS = H1 // P, H2 // P, NC // P
-W2_CHUNKS = 4
-W2_CHUNK_BLOCKS = H2_BLOCKS // W2_CHUNKS
-W3_CHUNKS = 8
-W3_CHUNK_BLOCKS = H2_BLOCKS // W3_CHUNKS
+HALVES = B // P
+CHUNK = 512
+CHUNKS = H2 // CHUNK
+CHUNK_BLOCKS = CHUNK // P
+W2_PIECES = 4
+W2_PIECE_CHUNKS = CHUNKS // W2_PIECES
 
-ROW_B2, ROW_GAIN2, ROW_SHIFT2 = 0, H2_BLOCKS, 2 * H2_BLOCKS
-ROW_B1 = 3 * H2_BLOCKS
+ROW_GAIN2, ROW_SHIFT2 = 0, H2_BLOCKS
+ROW_B1 = 2 * H2_BLOCKS
 ROW_GAIN1, ROW_SHIFT1, ROW_B3 = ROW_B1 + H1_BLOCKS, ROW_B1 + 2 * H1_BLOCKS, ROW_B1 + 3 * H1_BLOCKS
-
-LEAD = 2
 
 FLOPS = 2 * (D * H1 * N + H1 * H2 * B + H2 * NC * B)
 
@@ -34,9 +35,7 @@ def tile_ternarycreditrisknet_b_kernel(
     with (
         tc.tile_pool(name="held", bufs=1) as held,
         tc.tile_pool(name="work", bufs=4) as work,
-        tc.psum_pool(name="setup_ps", bufs=1) as setup_ps,
-        tc.psum_pool(name="stats_ps", bufs=1) as stats_ps,
-        tc.psum_pool(name="prod_ps", bufs=4) as prod_ps,
+        tc.psum_pool(name="banks", bufs=8) as banks,
     ):
         offsets = held.tile([P, N // 16], U16, name="offsets")
         nc.sync.dma_start(offsets[:], offs)
@@ -49,7 +48,7 @@ def tile_ternarycreditrisknet_b_kernel(
         nc.vector.memset(vector_rows[:], 0.0)
         for vector, row in (
             (b1, ROW_B1), (gain1, ROW_GAIN1), (shift1, ROW_SHIFT1),
-            (b2, ROW_B2), (gain2, ROW_GAIN2), (shift2, ROW_SHIFT2), (b3, ROW_B3),
+            (gain2, ROW_GAIN2), (shift2, ROW_SHIFT2), (b3, ROW_B3),
         ):
             blocks = vector.shape[0] // P
             nc.scalar.dma_start(
@@ -57,16 +56,18 @@ def tile_ternarycreditrisknet_b_kernel(
             )
 
         w2_view = w2.rearrange("(k p) u -> p k u", p=P)
-        w2_chunks = []
-        for c in range(W2_CHUNKS):
-            chunk = held.tile([P, H1_BLOCKS, H2 // W2_CHUNKS], BF16, name=f"w2_chunk{c}")
-            nc.sync.dma_start(chunk[:], w2_view[:, :, c * (H2 // W2_CHUNKS) : (c + 1) * (H2 // W2_CHUNKS)])
-            w2_chunks.append(chunk)
+        w2_pieces = []
+        for i in range(W2_PIECES):
+            piece = held.tile([P, H1_BLOCKS, H2 // W2_PIECES], BF16, name=f"w2_piece{i}")
+            nc.sync.dma_start(piece[:], w2_view[:, :, i * (H2 // W2_PIECES) : (i + 1) * (H2 // W2_PIECES)])
+            w2_pieces.append(piece)
+        b2_row = held.tile([P, H2], F32, name="b2_row")
+        nc.sync.dma_start(b2_row[:], b2.rearrange("u o -> (u o)").partition_broadcast(P))
         w3_view = w3.rearrange("(a p) q -> p a q", p=P)
         w3_chunks = []
-        for c in range(W3_CHUNKS):
-            chunk = held.tile([P, W3_CHUNK_BLOCKS, NC], BF16, name=f"w3_chunk{c}")
-            nc.sync.dma_start(chunk[:], w3_view[:, c * W3_CHUNK_BLOCKS : (c + 1) * W3_CHUNK_BLOCKS, :])
+        for c in range(CHUNKS):
+            chunk = held.tile([P, CHUNK_BLOCKS, NC], BF16, name=f"w3_chunk{c}")
+            nc.sync.dma_start(chunk[:], w3_view[:, c * CHUNK_BLOCKS : (c + 1) * CHUNK_BLOCKS, :])
             w3_chunks.append(chunk)
 
         identity_bf16 = held.tile([P, P], BF16, name="identity_bf16")
@@ -75,16 +76,16 @@ def tile_ternarycreditrisknet_b_kernel(
         make_identity(nc, identity_f32[:])
         mean_of_h1 = held.tile([P, P], F32, name="mean_of_h1")
         nc.vector.memset(mean_of_h1[:], 1.0 / H1)
-        mean_of_h2 = held.tile([P, P], F32, name="mean_of_h2")
-        nc.vector.memset(mean_of_h2[:], 1.0 / H2)
+        eps_column = held.tile([P, 1], F32, name="eps_column")
+        nc.vector.memset(eps_column[:], EPS)
 
-        table_ps = setup_ps.tile([D, V], BF16, name="table_ps")
+        table_ps = banks.tile([D, V], BF16, name="table_ps", tag="bank")
         for a in range(V // P):
             nc.tensor.transpose(table_ps[:, a * P : (a + 1) * P], table_rows[:, a, :], identity_bf16[:])
         window = held.tile([D, V], BF16, name="window")
         nc.vector.tensor_copy(window[:], table_ps[:])
 
-        vector_ps = setup_ps.tile([P, P], F32, name="vector_ps")
+        vector_ps = banks.tile([P, P], F32, name="vector_ps", tag="bank")
         nc.tensor.transpose(vector_ps[:], vector_rows[:], identity_f32[:])
         per_feature = held.tile([P, P], F32, name="per_feature")
         nc.vector.tensor_copy(per_feature[:], vector_ps[:])
@@ -92,116 +93,134 @@ def tile_ternarycreditrisknet_b_kernel(
         def column(row):
             return per_feature[:, row : row + 1]
 
-        def leave_psum(prod, scale, bias, y, sum_y, sum_sq):
-            nc.scalar.activation(y, prod[:], ACT.Identity, bias=bias, scale=scale)
-            square = work.tile([P, B], F32, name="square")
-            nc.scalar.activation(square[:], prod[:], ACT.Square, bias=bias, scale=scale)
-            nc.vector.tensor_tensor(sum_y[:], sum_y[:], y, ALU.add)
-            nc.vector.tensor_tensor(sum_sq[:], sum_sq[:], square[:], ALU.add)
-
-        def statistics(sum_y, sum_sq, mean_weights, layer):
-            mean = stats_ps.tile([P, B], F32, name="mean")
-            nc.tensor.matmul(mean[:], mean_weights[:], sum_y[:], start=True, stop=True)
-            mean_sq = stats_ps.tile([P, B], F32, name="mean_sq")
-            nc.tensor.matmul(mean_sq[:], mean_weights[:], sum_sq[:], start=True, stop=True)
-            square_of_mean = work.tile([P, B], F32, name="square_of_mean")
-            nc.scalar.activation(square_of_mean[:], mean[:], ACT.Square)
-            var_eps = work.tile([P, B], F32, name="var_eps")
-            nc.vector.scalar_tensor_tensor(
-                var_eps[:], mean_sq[:], EPS, square_of_mean[:], op0=ALU.add, op1=ALU.subtract
-            )
-            rstd = held.tile([P, B], F32, name=f"rstd{layer}")
-            nc.scalar.activation(rstd[:], var_eps[:], ACT.Abs_reciprocal_sqrt)
-            return mean, rstd
-
-        def norm_gelu(y, mean, rstd, gain_row, shift_row, new_h, use_h):
-            mean_twice = mean[:].unsqueeze(1).to_broadcast([P, 2, B])
-            rstd_twice = rstd[:].unsqueeze(1).to_broadcast([P, 2, B])
-            centred = []
-
-            def centre(g):
-                centred.append(work.tile([P, 2, B], F32, name="centred"))
-                nc.vector.tensor_tensor(centred[g][:], y[g][:], mean_twice, ALU.subtract)
-
-            for g in range(LEAD):
-                centre(g)
-            for g in range(len(y)):
-                if g + LEAD < len(y):
-                    centre(g + LEAD)
-                nc.vector.tensor_tensor(centred[g][:], centred[g][:], rstd_twice, ALU.mult)
-                for i in range(2):
-                    a = 2 * g + i
-                    h = new_h(a)
-                    nc.scalar.activation(
-                        h[:], centred[g][:, i, :], ACT.Gelu,
-                        bias=column(shift_row + a), scale=column(gain_row + a),
-                    )
-                    use_h(a, h)
-
         def load_rsqrt_table(after):
             unused = work.tile([P, 1], F32, name="unused")
             nc.scalar.activation(unused[:], after, ACT.Abs_reciprocal_sqrt, bias=1.0, scale=0.0)
 
         sum_y1 = held.tile([P, B], F32, name="sum_y1")
         sum_sq1 = held.tile([P, B], F32, name="sum_sq1")
-        sum_y2 = held.tile([P, B], F32, name="sum_y2")
-        sum_sq2 = held.tile([P, B], F32, name="sum_sq2")
-        for sums in (sum_y1, sum_sq1, sum_y2, sum_sq2):
+        for sums in (sum_y1, sum_sq1):
             nc.vector.memset(sums[:], 0.0)
 
         load_rsqrt_table(after=sum_y1[:, 0:1])
-        y1 = []
+        y1 = [held.tile([P, 2, B], F32, name=f"y1_{g}") for g in range(H1_BLOCKS // 2)]
         for a in range(H1_BLOCKS):
-            prod = prod_ps.tile([P, B], F32, name="prod")
+            prod1 = banks.tile([P, B], F32, name="prod1", tag="bank")
             for t in range(T):
                 nc.tensor.matmul(
-                    prod[:],
+                    prod1[:],
                     w1_sb[:, a * P : (a + 1) * P],
                     window[:].indirect(offsets[:, t * (B // 16) : (t + 1) * (B // 16)]),
                     start=(t == 0),
                     stop=(t == T - 1),
                 )
-            if a % 2 == 0:
-                y1.append(held.tile([P, 2, B], F32, name=f"y1_{a // 2}"))
-            leave_psum(prod, QS / T, column(ROW_B1 + a), y1[a // 2][:, a % 2, :], sum_y1, sum_sq1)
-        mean1, rstd1 = statistics(sum_y1, sum_sq1, mean_of_h1, 1)
-        h1 = []
-        norm_gelu(
-            y1, mean1, rstd1, ROW_GAIN1, ROW_SHIFT1,
-            new_h=lambda a: held.tile([P, B], BF16, name=f"h1_{a}"),
-            use_h=lambda a, h: h1.append(h),
-        )
+            y1_block = y1[a // 2][:, a % 2, :]
+            nc.scalar.activation(y1_block, prod1[:], ACT.Identity, bias=column(ROW_B1 + a), scale=QS / T)
+            square1 = work.tile([P, B], F32, name="square1")
+            nc.scalar.activation(square1[:], prod1[:], ACT.Square, bias=column(ROW_B1 + a), scale=QS / T)
+            nc.vector.tensor_tensor(sum_y1[:], sum_y1[:], y1_block, ALU.add)
+            nc.vector.tensor_tensor(sum_sq1[:], sum_sq1[:], square1[:], ALU.add)
 
-        y2 = []
-        for a in range(H2_BLOCKS):
-            chunk, j = w2_chunks[a // W2_CHUNK_BLOCKS], a % W2_CHUNK_BLOCKS
-            prod = prod_ps.tile([P, B], F32, name="prod")
+        mean1 = banks.tile([P, B], F32, name="mean1", tag="bank")
+        nc.tensor.matmul(mean1[:], mean_of_h1[:], sum_y1[:], start=True, stop=True)
+        mean_sq1 = banks.tile([P, B], F32, name="mean_sq1", tag="bank")
+        nc.tensor.matmul(mean_sq1[:], mean_of_h1[:], sum_sq1[:], start=True, stop=True)
+        square_of_mean1 = work.tile([P, B], F32, name="square_of_mean1")
+        nc.scalar.activation(square_of_mean1[:], mean1[:], ACT.Square)
+        var_eps1 = work.tile([P, B], F32, name="var_eps1")
+        nc.vector.scalar_tensor_tensor(
+            var_eps1[:], mean_sq1[:], EPS, square_of_mean1[:], op0=ALU.add, op1=ALU.subtract
+        )
+        rstd1 = held.tile([P, B], F32, name="rstd1")
+        nc.scalar.activation(rstd1[:], var_eps1[:], ACT.Abs_reciprocal_sqrt)
+
+        for g in range(H1_BLOCKS // 2):
+            nc.vector.tensor_tensor(y1[g][:], y1[g][:], mean1[:].unsqueeze(1).to_broadcast([P, 2, B]), ALU.subtract)
+        h1 = []
+        for g in range(H1_BLOCKS // 2):
+            nc.vector.tensor_tensor(y1[g][:], y1[g][:], rstd1[:].unsqueeze(1).to_broadcast([P, 2, B]), ALU.mult)
+            for i in range(2):
+                a = 2 * g + i
+                h1.append(held.tile([P, B], BF16, name=f"h1_{a}"))
+                nc.scalar.activation(
+                    h1[a][:], y1[g][:, i, :], ACT.Gelu,
+                    bias=column(ROW_SHIFT1 + a), scale=column(ROW_GAIN1 + a),
+                )
+        load_rsqrt_table(after=h1[H1_BLOCKS - 1][:, 0:1])
+
+        y2 = [[held.tile([P, CHUNK], F32, name=f"y2_{half}_{c}") for c in range(CHUNKS)] for half in range(HALVES)]
+        h2 = [[held.tile([P, P], BF16, name=f"h2_{half}_{a}") for a in range(H2_BLOCKS)] for half in range(HALVES)]
+        sums = [held.tile([P, CHUNKS], F32, name=f"sums{half}") for half in range(HALVES)]
+        sq_sums = [held.tile([P, CHUNKS], F32, name=f"sq_sums{half}") for half in range(HALVES)]
+        neg_mean = [held.tile([P, 1], F32, name=f"neg_mean{half}") for half in range(HALVES)]
+        rstd2 = [held.tile([P, 1], F32, name=f"rstd2_{half}") for half in range(HALVES)]
+        out_ps = [banks.tile([P, B], F32, name=f"out_ps{q}", tag="bank") for q in range(NC_BLOCKS)]
+
+        def layer2(half, c):
+            piece, i = w2_pieces[c // W2_PIECE_CHUNKS], c % W2_PIECE_CHUNKS
+            prod2 = banks.tile([P, CHUNK], F32, name="prod2", tag="bank")
             for k in range(H1_BLOCKS):
                 nc.tensor.matmul(
-                    prod[:], chunk[:, k, j * P : (j + 1) * P], h1[k][:],
+                    prod2[:], h1[k][:, half * P : (half + 1) * P], piece[:, k, i * CHUNK : (i + 1) * CHUNK],
                     start=(k == 0), stop=(k == H1_BLOCKS - 1),
                 )
-            if a % 2 == 0:
-                y2.append(held.tile([P, 2, B], F32, name=f"y2_{a // 2}"))
-            leave_psum(prod, QS, column(ROW_B2 + a), y2[a // 2][:, a % 2, :], sum_y2, sum_sq2)
-        load_rsqrt_table(after=y2[H2_BLOCKS // 2 - 1][:, 1, 0:1])
-        mean2, rstd2 = statistics(sum_y2, sum_sq2, mean_of_h2, 2)
+            nc.vector.scalar_tensor_tensor(
+                y2[half][c][:], prod2[:], QS, b2_row[:, c * CHUNK : (c + 1) * CHUNK],
+                op0=ALU.mult, op1=ALU.add, accum_out=sums[half][:, c : c + 1],
+            )
+            squares = work.tile([P, CHUNK], BF16, name="squares")
+            nc.scalar.activation(squares[:], y2[half][c][:], ACT.Square, accum_out=sq_sums[half][:, c : c + 1])
 
-        out_ps = [prod_ps.tile([P, B], F32, name=f"out_ps{q}", tag="prod") for q in range(NC_BLOCKS)]
+        def statistics(half):
+            total = work.tile([P, 1], F32, name="total")
+            nc.vector.reduce_sum(total[:], sums[half][:], axis=ALONG_FREE)
+            nc.vector.tensor_scalar_mul(neg_mean[half][:], total[:], -1.0 / H2)
+            total_sq = work.tile([P, 1], F32, name="total_sq")
+            nc.vector.reduce_sum(total_sq[:], sq_sums[half][:], axis=ALONG_FREE)
+            square_of_mean = work.tile([P, 1], F32, name="square_of_mean")
+            nc.vector.tensor_tensor(square_of_mean[:], neg_mean[half][:], neg_mean[half][:], ALU.mult)
+            var = work.tile([P, 1], F32, name="var")
+            nc.vector.scalar_tensor_tensor(
+                var[:], total_sq[:], 1.0 / H2, square_of_mean[:], op0=ALU.mult, op1=ALU.subtract
+            )
+            nc.scalar.activation(rstd2[half][:], var[:], ACT.Abs_reciprocal_sqrt, bias=eps_column[:], scale=1.0)
 
-        def layer3(a, h2):
-            chunk, j = w3_chunks[a // W3_CHUNK_BLOCKS], a % W3_CHUNK_BLOCKS
-            for q in range(NC_BLOCKS):
-                nc.tensor.matmul(
-                    out_ps[q][:], chunk[:, j, q * P : (q + 1) * P], h2[:],
-                    start=(a == 0), stop=(a == H2_BLOCKS - 1),
+        def norm_gelu(half, c):
+            normed = y2[half][c]
+            nc.vector.tensor_scalar(
+                normed[:], normed[:], neg_mean[half][:], rstd2[half][:], op0=ALU.add, op1=ALU.mult
+            )
+            flipped = banks.tile([P, CHUNK_BLOCKS, P], F32, name="flipped", tag="bank")
+            for j in range(CHUNK_BLOCKS):
+                nc.tensor.transpose(flipped[:, j, :], normed[:, j * P : (j + 1) * P], identity_f32[:])
+            for j in range(CHUNK_BLOCKS):
+                a = c * CHUNK_BLOCKS + j
+                nc.scalar.activation(
+                    h2[half][a][:], flipped[:, j, :], ACT.Gelu,
+                    bias=column(ROW_SHIFT2 + a), scale=column(ROW_GAIN2 + a),
                 )
 
-        norm_gelu(
-            y2, mean2, rstd2, ROW_GAIN2, ROW_SHIFT2,
-            new_h=lambda a: work.tile([P, B], BF16, name="h2"),
-            use_h=layer3,
-        )
+        def layer3(half, c):
+            for j in range(CHUNK_BLOCKS):
+                a = c * CHUNK_BLOCKS + j
+                for q in range(NC_BLOCKS):
+                    nc.tensor.matmul(
+                        out_ps[q][:, half * P : (half + 1) * P], w3_chunks[c][:, j, q * P : (q + 1) * P], h2[half][a][:],
+                        start=(a == 0), stop=(a == H2_BLOCKS - 1),
+                    )
+
+        for c in range(CHUNKS):
+            layer2(0, c)
+        statistics(0)
+        for c in range(CHUNKS):
+            layer2(1, c)
+            norm_gelu(0, c)
+        statistics(1)
+        for c in range(CHUNKS):
+            layer3(0, c)
+            norm_gelu(1, c)
+        for c in range(CHUNKS):
+            layer3(1, c)
 
         for q in range(NC_BLOCKS):
             out_sb = work.tile([P, B], F32, name="out_sb")

@@ -20,6 +20,7 @@ CHUNKS = H2 // CHUNK
 CHUNK_BLOCKS = CHUNK // P
 W2_PIECES = 4
 W2_PIECE_CHUNKS = CHUNKS // W2_PIECES
+LEAD = 2
 
 ROW_GAIN2, ROW_SHIFT2 = 0, H2_BLOCKS
 ROW_B1 = 2 * H2_BLOCKS
@@ -76,8 +77,8 @@ def tile_ternarycreditrisknet_b_kernel(
         make_identity(nc, identity_f32[:])
         mean_of_h1 = held.tile([P, P], F32, name="mean_of_h1")
         nc.vector.memset(mean_of_h1[:], 1.0 / H1)
-        eps_column = held.tile([P, 1], F32, name="eps_column")
-        nc.vector.memset(eps_column[:], EPS)
+        minus_half = held.tile([P, 1], F32, name="minus_half")
+        nc.vector.memset(minus_half[:], -0.5)
 
         table_ps = banks.tile([D, V], BF16, name="table_ps", tag="bank")
         for a in range(V // P):
@@ -93,16 +94,13 @@ def tile_ternarycreditrisknet_b_kernel(
         def column(row):
             return per_feature[:, row : row + 1]
 
-        def load_rsqrt_table(after):
-            unused = work.tile([P, 1], F32, name="unused")
-            nc.scalar.activation(unused[:], after, ACT.Abs_reciprocal_sqrt, bias=1.0, scale=0.0)
-
         sum_y1 = held.tile([P, B], F32, name="sum_y1")
         sum_sq1 = held.tile([P, B], F32, name="sum_sq1")
         for sums in (sum_y1, sum_sq1):
             nc.vector.memset(sums[:], 0.0)
 
-        load_rsqrt_table(after=sum_y1[:, 0:1])
+        unused = work.tile([P, 1], F32, name="unused")
+        nc.scalar.activation(unused[:], sum_y1[:, 0:1], ACT.Abs_reciprocal_sqrt, bias=1.0, scale=0.0)
         y1 = [held.tile([P, 2, B], F32, name=f"y1_{g}") for g in range(H1_BLOCKS // 2)]
         for a in range(H1_BLOCKS):
             prod1 = banks.tile([P, B], F32, name="prod1", tag="bank")
@@ -146,7 +144,6 @@ def tile_ternarycreditrisknet_b_kernel(
                     h1[a][:], y1[g][:, i, :], ACT.Gelu,
                     bias=column(ROW_SHIFT1 + a), scale=column(ROW_GAIN1 + a),
                 )
-        load_rsqrt_table(after=h1[H1_BLOCKS - 1][:, 0:1])
 
         y2 = [[held.tile([P, CHUNK], F32, name=f"y2_{half}_{c}") for c in range(CHUNKS)] for half in range(HALVES)]
         h2 = [[held.tile([P, P], BF16, name=f"h2_{half}_{a}") for a in range(H2_BLOCKS)] for half in range(HALVES)]
@@ -183,7 +180,9 @@ def tile_ternarycreditrisknet_b_kernel(
             nc.vector.scalar_tensor_tensor(
                 var[:], total_sq[:], 1.0 / H2, square_of_mean[:], op0=ALU.mult, op1=ALU.subtract
             )
-            nc.scalar.activation(rstd2[half][:], var[:], ACT.Abs_reciprocal_sqrt, bias=eps_column[:], scale=1.0)
+            var_eps = work.tile([P, 1], F32, name="var_eps")
+            nc.vector.tensor_scalar(var_eps[:], var[:], 0.0, EPS, op0=ALU.max, op1=ALU.add)
+            nc.gpsimd.tensor_tensor(rstd2[half][:], var_eps[:], minus_half[:], ALU.pow)
 
         def norm_gelu(half, c):
             normed = y2[half][c]
@@ -201,26 +200,27 @@ def tile_ternarycreditrisknet_b_kernel(
                 )
 
         def layer3(half, c):
-            for j in range(CHUNK_BLOCKS):
-                a = c * CHUNK_BLOCKS + j
-                for q in range(NC_BLOCKS):
+            for q in range(NC_BLOCKS):
+                for j in range(CHUNK_BLOCKS):
+                    a = c * CHUNK_BLOCKS + j
                     nc.tensor.matmul(
                         out_ps[q][:, half * P : (half + 1) * P], w3_chunks[c][:, j, q * P : (q + 1) * P], h2[half][a][:],
                         start=(a == 0), stop=(a == H2_BLOCKS - 1),
                     )
 
+        units = [(half, c) for half in range(HALVES) for c in range(CHUNKS)]
         for c in range(CHUNKS):
             layer2(0, c)
         statistics(0)
         for c in range(CHUNKS):
+            if c >= CHUNKS - LEAD:
+                norm_gelu(*units[c - (CHUNKS - LEAD)])
             layer2(1, c)
-            norm_gelu(0, c)
         statistics(1)
-        for c in range(CHUNKS):
-            layer3(0, c)
-            norm_gelu(1, c)
-        for c in range(CHUNKS):
-            layer3(1, c)
+        for i, unit in enumerate(units):
+            if i + LEAD < len(units):
+                norm_gelu(*units[i + LEAD])
+            layer3(*unit)
 
         for q in range(NC_BLOCKS):
             out_sb = work.tile([P, B], F32, name="out_sb")

@@ -38,12 +38,12 @@ def tile_ternarycreditrisknet_b_kernel(
         tc.tile_pool(name="work", bufs=4) as work,
         tc.psum_pool(name="banks", bufs=8) as banks,
     ):
-        offsets = held.tile([P, N // 16], U16, name="offsets")
-        nc.sync.dma_start(offsets[:], offs)
         table_rows = held.tile([P, V // P, D], BF16, name="table_rows")
         nc.sync.dma_start(table_rows[:], table.rearrange("(a p) d -> p a d", p=P))
+        offsets = held.tile([P, N // 16], U16, name="offsets")
+        nc.sync.dma_start(offsets[:], offs)
         w1_sb = held.tile([D, H1], BF16, name="w1_sb")
-        nc.scalar.dma_start(w1_sb[:], w1)
+        nc.sync.dma_start(w1_sb[:], w1)
 
         vector_rows = held.tile([P, P], F32, name="vector_rows")
         nc.vector.memset(vector_rows[:], 0.0)
@@ -52,7 +52,7 @@ def tile_ternarycreditrisknet_b_kernel(
             (gain2, ROW_GAIN2), (shift2, ROW_SHIFT2), (b3, ROW_B3),
         ):
             blocks = vector.shape[0] // P
-            nc.scalar.dma_start(
+            nc.sync.dma_start(
                 vector_rows[row : row + blocks, :], vector.rearrange("(a p) o -> a (p o)", p=P)
             )
 
@@ -119,31 +119,38 @@ def tile_ternarycreditrisknet_b_kernel(
             nc.vector.tensor_tensor(sum_y1[:], sum_y1[:], y1_block, ALU.add)
             nc.vector.tensor_tensor(sum_sq1[:], sum_sq1[:], square1[:], ALU.add)
 
-        mean1 = banks.tile([P, B], F32, name="mean1", tag="bank")
-        nc.tensor.matmul(mean1[:], mean_of_h1[:], sum_y1[:], start=True, stop=True)
-        mean_sq1 = banks.tile([P, B], F32, name="mean_sq1", tag="bank")
-        nc.tensor.matmul(mean_sq1[:], mean_of_h1[:], sum_sq1[:], start=True, stop=True)
-        square_of_mean1 = work.tile([P, B], F32, name="square_of_mean1")
-        nc.scalar.activation(square_of_mean1[:], mean1[:], ACT.Square)
-        var_eps1 = work.tile([P, B], F32, name="var_eps1")
-        nc.vector.scalar_tensor_tensor(
-            var_eps1[:], mean_sq1[:], EPS, square_of_mean1[:], op0=ALU.add, op1=ALU.subtract
-        )
-        rstd1 = held.tile([P, B], F32, name="rstd1")
-        nc.scalar.activation(rstd1[:], var_eps1[:], ACT.Abs_reciprocal_sqrt)
+        h1 = [held.tile([P, B], BF16, name=f"h1_{a}") for a in range(H1_BLOCKS)]
+        for half in range(HALVES):
+            records = slice(half * P, (half + 1) * P)
+            mean1 = banks.tile([P, P], F32, name="mean1", tag="bank")
+            nc.tensor.matmul(mean1[:], mean_of_h1[:], sum_y1[:, records], start=True, stop=True)
+            mean_sq1 = banks.tile([P, P], F32, name="mean_sq1", tag="bank")
+            nc.tensor.matmul(mean_sq1[:], mean_of_h1[:], sum_sq1[:, records], start=True, stop=True)
+            square_of_mean1 = work.tile([P, P], F32, name="square_of_mean1")
+            nc.scalar.activation(square_of_mean1[:], mean1[:], ACT.Square)
+            var_eps1 = work.tile([P, P], F32, name="var_eps1")
+            nc.vector.scalar_tensor_tensor(
+                var_eps1[:], mean_sq1[:], EPS, square_of_mean1[:], op0=ALU.add, op1=ALU.subtract
+            )
+            rstd1 = work.tile([P, P], F32, name="rstd1")
+            nc.scalar.activation(rstd1[:], var_eps1[:], ACT.Abs_reciprocal_sqrt)
 
-        for g in range(H1_BLOCKS // 2):
-            nc.vector.tensor_tensor(y1[g][:], y1[g][:], mean1[:].unsqueeze(1).to_broadcast([P, 2, B]), ALU.subtract)
-        h1 = []
-        for g in range(H1_BLOCKS // 2):
-            nc.vector.tensor_tensor(y1[g][:], y1[g][:], rstd1[:].unsqueeze(1).to_broadcast([P, 2, B]), ALU.mult)
-            for i in range(2):
-                a = 2 * g + i
-                h1.append(held.tile([P, B], BF16, name=f"h1_{a}"))
-                nc.scalar.activation(
-                    h1[a][:], y1[g][:, i, :], ACT.Gelu,
-                    bias=column(ROW_SHIFT1 + a), scale=column(ROW_GAIN1 + a),
+            for g in range(H1_BLOCKS // 2):
+                nc.vector.tensor_tensor(
+                    y1[g][:, :, records], y1[g][:, :, records],
+                    mean1[:].unsqueeze(1).to_broadcast([P, 2, P]), ALU.subtract,
                 )
+            for g in range(H1_BLOCKS // 2):
+                nc.vector.tensor_tensor(
+                    y1[g][:, :, records], y1[g][:, :, records],
+                    rstd1[:].unsqueeze(1).to_broadcast([P, 2, P]), ALU.mult,
+                )
+                for i in range(2):
+                    a = 2 * g + i
+                    nc.scalar.activation(
+                        h1[a][:, records], y1[g][:, i, records], ACT.Gelu,
+                        bias=column(ROW_SHIFT1 + a), scale=column(ROW_GAIN1 + a),
+                    )
 
         y2 = [[held.tile([P, CHUNK], F32, name=f"y2_{half}_{c}") for c in range(CHUNKS)] for half in range(HALVES)]
         h2 = [[held.tile([P, P], BF16, name=f"h2_{half}_{a}") for a in range(H2_BLOCKS)] for half in range(HALVES)]

@@ -22,10 +22,6 @@ W2_PIECES = 4
 W2_PIECE_CHUNKS = CHUNKS // W2_PIECES
 LEAD = 2
 
-ROW_GAIN2, ROW_SHIFT2 = 0, H2_BLOCKS
-ROW_B1 = 2 * H2_BLOCKS
-ROW_GAIN1, ROW_SHIFT1, ROW_B3 = ROW_B1 + H1_BLOCKS, ROW_B1 + 2 * H1_BLOCKS, ROW_B1 + 3 * H1_BLOCKS
-
 FLOPS = 2 * (D * H1 * N + H1 * H2 * B + H2 * NC * B)
 
 
@@ -45,16 +41,14 @@ def tile_ternarycreditrisknet_b_kernel(
         w1_sb = held.tile([D, H1], BF16, name="w1_sb")
         nc.sync.dma_start(w1_sb[:], w1)
 
-        vector_rows = held.tile([P, P], F32, name="vector_rows")
-        nc.vector.memset(vector_rows[:], 0.0)
-        for vector, row in (
-            (b1, ROW_B1), (gain1, ROW_GAIN1), (shift1, ROW_SHIFT1),
-            (gain2, ROW_GAIN2), (shift2, ROW_SHIFT2), (b3, ROW_B3),
-        ):
-            blocks = vector.shape[0] // P
-            nc.sync.dma_start(
-                vector_rows[row : row + blocks, :], vector.rearrange("(a p) o -> a (p o)", p=P)
-            )
+        def load_columns(vector, name):
+            columns = held.tile([P, vector.shape[0] // P], F32, name=name)
+            nc.sync.dma_start(columns[:], vector.rearrange("(a p) o -> p (a o)", p=P))
+            return columns
+
+        b1_sb = load_columns(b1, "b1_sb")
+        gain1_sb = load_columns(gain1, "gain1_sb")
+        shift1_sb = load_columns(shift1, "shift1_sb")
 
         w2_view = w2.rearrange("(k p) u -> p k u", p=P)
         w2_pieces = []
@@ -64,6 +58,9 @@ def tile_ternarycreditrisknet_b_kernel(
             w2_pieces.append(piece)
         b2_row = held.tile([P, H2], F32, name="b2_row")
         nc.sync.dma_start(b2_row[:], b2.rearrange("u o -> (u o)").partition_broadcast(P))
+        gain2_sb = load_columns(gain2, "gain2_sb")
+        shift2_sb = load_columns(shift2, "shift2_sb")
+        b3_sb = load_columns(b3, "b3_sb")
         w3_view = w3.rearrange("(a p) q -> p a q", p=P)
         w3_chunks = []
         for c in range(CHUNKS):
@@ -86,14 +83,6 @@ def tile_ternarycreditrisknet_b_kernel(
         window = held.tile([D, V], BF16, name="window")
         nc.vector.tensor_copy(window[:], table_ps[:])
 
-        vector_ps = banks.tile([P, P], F32, name="vector_ps", tag="bank")
-        nc.tensor.transpose(vector_ps[:], vector_rows[:], identity_f32[:])
-        per_feature = held.tile([P, P], F32, name="per_feature")
-        nc.vector.tensor_copy(per_feature[:], vector_ps[:])
-
-        def column(row):
-            return per_feature[:, row : row + 1]
-
         sum_y1 = held.tile([P, B], F32, name="sum_y1")
         sum_sq1 = held.tile([P, B], F32, name="sum_sq1")
         for sums in (sum_y1, sum_sq1):
@@ -112,12 +101,16 @@ def tile_ternarycreditrisknet_b_kernel(
                     start=(t == 0),
                     stop=(t == T - 1),
                 )
-            y1_block = y1[a // 2][:, a % 2, :]
-            nc.scalar.activation(y1_block, prod1[:], ACT.Identity, bias=column(ROW_B1 + a), scale=QS / T)
             square1 = work.tile([P, B], F32, name="square1")
-            nc.scalar.activation(square1[:], prod1[:], ACT.Square, bias=column(ROW_B1 + a), scale=QS / T)
-            nc.vector.tensor_tensor(sum_y1[:], sum_y1[:], y1_block, ALU.add)
-            nc.vector.tensor_tensor(sum_sq1[:], sum_sq1[:], square1[:], ALU.add)
+            for half in range(HALVES):
+                records = slice(half * P, (half + 1) * P)
+                y1_block = y1[a // 2][:, a % 2, records]
+                nc.scalar.activation(y1_block, prod1[:, records], ACT.Identity, bias=b1_sb[:, a : a + 1], scale=QS / T)
+                nc.scalar.activation(
+                    square1[:, records], prod1[:, records], ACT.Square, bias=b1_sb[:, a : a + 1], scale=QS / T
+                )
+                nc.vector.tensor_tensor(sum_y1[:, records], sum_y1[:, records], y1_block, ALU.add)
+                nc.vector.tensor_tensor(sum_sq1[:, records], sum_sq1[:, records], square1[:, records], ALU.add)
 
         h1 = [held.tile([P, B], BF16, name=f"h1_{a}") for a in range(H1_BLOCKS)]
         for half in range(HALVES):
@@ -149,7 +142,7 @@ def tile_ternarycreditrisknet_b_kernel(
                     a = 2 * g + i
                     nc.scalar.activation(
                         h1[a][:, records], y1[g][:, i, records], ACT.Gelu,
-                        bias=column(ROW_SHIFT1 + a), scale=column(ROW_GAIN1 + a),
+                        bias=shift1_sb[:, a : a + 1], scale=gain1_sb[:, a : a + 1],
                     )
 
         y2 = [[held.tile([P, CHUNK], F32, name=f"y2_{half}_{c}") for c in range(CHUNKS)] for half in range(HALVES)]
@@ -203,7 +196,7 @@ def tile_ternarycreditrisknet_b_kernel(
                 a = c * CHUNK_BLOCKS + j
                 nc.scalar.activation(
                     h2[half][a][:], flipped[:, j, :], ACT.Gelu,
-                    bias=column(ROW_SHIFT2 + a), scale=column(ROW_GAIN2 + a),
+                    bias=shift2_sb[:, a : a + 1], scale=gain2_sb[:, a : a + 1],
                 )
 
         def layer3(half, c):
@@ -232,8 +225,8 @@ def tile_ternarycreditrisknet_b_kernel(
         for q in range(NC_BLOCKS):
             out_sb = work.tile([P, B], F32, name="out_sb")
             if q % 2 == 0:
-                nc.scalar.activation(out_sb[:], out_ps[q][:], ACT.Identity, bias=column(ROW_B3 + q), scale=QS)
+                nc.scalar.activation(out_sb[:], out_ps[q][:], ACT.Identity, bias=b3_sb[:, q : q + 1], scale=QS)
                 nc.sync.dma_start(out[q * P : (q + 1) * P, :], out_sb[:])
             else:
-                nc.vector.tensor_scalar(out_sb[:], out_ps[q][:], QS, column(ROW_B3 + q), op0=ALU.mult, op1=ALU.add)
+                nc.vector.tensor_scalar(out_sb[:], out_ps[q][:], QS, b3_sb[:, q : q + 1], op0=ALU.mult, op1=ALU.add)
                 nc.scalar.dma_start(out[q * P : (q + 1) * P, :], out_sb[:])

@@ -77,11 +77,11 @@ def tile_ternarycreditrisknet_b_kernel(
         minus_half = held.tile([P, 1], F32, name="minus_half")
         nc.vector.memset(minus_half[:], -0.5)
 
-        table_ps = banks.tile([D, V], BF16, name="table_ps", tag="bank")
-        for a in range(V // P):
-            nc.tensor.transpose(table_ps[:, a * P : (a + 1) * P], table_rows[:, a, :], identity_bf16[:])
         window = held.tile([D, V], BF16, name="window")
-        nc.vector.tensor_copy(window[:], table_ps[:])
+        for a in range(V // P):
+            words_ps = banks.tile([D, P], BF16, name="words_ps", tag="bank")
+            nc.tensor.transpose(words_ps[:], table_rows[:, a, :], identity_bf16[:])
+            nc.vector.tensor_copy(window[:, a * P : (a + 1) * P], words_ps[:])
 
         sum_y1 = held.tile([P, B], F32, name="sum_y1")
         sum_sq1 = held.tile([P, B], F32, name="sum_sq1")
@@ -91,30 +91,34 @@ def tile_ternarycreditrisknet_b_kernel(
         unused = work.tile([P, 1], F32, name="unused")
         nc.scalar.activation(unused[:], sum_y1[:, 0:1], ACT.Abs_reciprocal_sqrt, bias=1.0, scale=0.0)
         y1 = [held.tile([P, 2, B], F32, name=f"y1_{g}") for g in range(H1_BLOCKS // 2)]
+        prod1 = [banks.tile([P, B], F32, name=f"prod1_{a}", tag="bank") for a in range(H1_BLOCKS)]
+
+        def leave_psum1(a, half):
+            records = slice(half * P, (half + 1) * P)
+            y1_block = y1[a // 2][:, a % 2, records]
+            nc.scalar.activation(y1_block, prod1[a][:, records], ACT.Identity, bias=b1_sb[:, a : a + 1], scale=QS / T)
+            square1 = work.tile([P, P], F32, name="square1")
+            nc.scalar.activation(square1[:], prod1[a][:, records], ACT.Square, bias=b1_sb[:, a : a + 1], scale=QS / T)
+            nc.vector.tensor_tensor(sum_y1[:, records], sum_y1[:, records], y1_block, ALU.add)
+            nc.vector.tensor_tensor(sum_sq1[:, records], sum_sq1[:, records], square1[:], ALU.add)
+
         for a in range(H1_BLOCKS):
-            prod1 = banks.tile([P, B], F32, name="prod1", tag="bank")
             for t in range(T):
                 nc.tensor.matmul(
-                    prod1[:],
+                    prod1[a][:],
                     w1_sb[:, a * P : (a + 1) * P],
                     window[:].indirect(offsets[:, t * (B // 16) : (t + 1) * (B // 16)]),
                     start=(t == 0),
                     stop=(t == T - 1),
                 )
-            square1 = work.tile([P, B], F32, name="square1")
-            for half in range(HALVES):
-                records = slice(half * P, (half + 1) * P)
-                y1_block = y1[a // 2][:, a % 2, records]
-                nc.scalar.activation(y1_block, prod1[:, records], ACT.Identity, bias=b1_sb[:, a : a + 1], scale=QS / T)
-                nc.scalar.activation(
-                    square1[:, records], prod1[:, records], ACT.Square, bias=b1_sb[:, a : a + 1], scale=QS / T
-                )
-                nc.vector.tensor_tensor(sum_y1[:, records], sum_y1[:, records], y1_block, ALU.add)
-                nc.vector.tensor_tensor(sum_sq1[:, records], sum_sq1[:, records], square1[:, records], ALU.add)
+            leave_psum1(a, 0)
 
         h1 = [held.tile([P, B], BF16, name=f"h1_{a}") for a in range(H1_BLOCKS)]
         for half in range(HALVES):
             records = slice(half * P, (half + 1) * P)
+            if half > 0:
+                for a in range(H1_BLOCKS):
+                    leave_psum1(a, half)
             mean1 = banks.tile([P, P], F32, name="mean1", tag="bank")
             nc.tensor.matmul(mean1[:], mean_of_h1[:], sum_y1[:, records], start=True, stop=True)
             mean_sq1 = banks.tile([P, P], F32, name="mean_sq1", tag="bank")

@@ -20,7 +20,7 @@ CHUNKS = H2 // CHUNK
 CHUNK_BLOCKS = CHUNK // P
 W2_PIECES = 4
 W2_PIECE_CHUNKS = CHUNKS // W2_PIECES
-LEAD = 2
+LEAD = 3
 
 FLOPS = 2 * (D * H1 * N + H1 * H2 * B + H2 * NC * B)
 

@@ -212,6 +212,21 @@ def tile_ternarycreditrisknet_b_kernel(
                         start=(a == 0), stop=(a == H2_BLOCKS - 1),
                     )
 
+        def leave_psum3(half):
+            records = slice(half * P, (half + 1) * P)
+            for q in range(NC_BLOCKS):
+                out_sb = work.tile([P, P], F32, name="out_sb")
+                if q % 2 == 0:
+                    nc.scalar.activation(
+                        out_sb[:], out_ps[q][:, records], ACT.Identity, bias=b3_sb[:, q : q + 1], scale=QS
+                    )
+                    nc.sync.dma_start(out[q * P : (q + 1) * P, records], out_sb[:])
+                else:
+                    nc.vector.tensor_scalar(
+                        out_sb[:], out_ps[q][:, records], QS, b3_sb[:, q : q + 1], op0=ALU.mult, op1=ALU.add
+                    )
+                    nc.scalar.dma_start(out[q * P : (q + 1) * P, records], out_sb[:])
+
         units = [(half, c) for half in range(HALVES) for c in range(CHUNKS)]
         for c in range(CHUNKS):
             layer2(0, c)
@@ -225,12 +240,5 @@ def tile_ternarycreditrisknet_b_kernel(
             if i + LEAD < len(units):
                 norm_gelu(*units[i + LEAD])
             layer3(*unit)
-
-        for q in range(NC_BLOCKS):
-            out_sb = work.tile([P, B], F32, name="out_sb")
-            if q % 2 == 0:
-                nc.scalar.activation(out_sb[:], out_ps[q][:], ACT.Identity, bias=b3_sb[:, q : q + 1], scale=QS)
-                nc.sync.dma_start(out[q * P : (q + 1) * P, :], out_sb[:])
-            else:
-                nc.vector.tensor_scalar(out_sb[:], out_ps[q][:], QS, b3_sb[:, q : q + 1], op0=ALU.mult, op1=ALU.add)
-                nc.scalar.dma_start(out[q * P : (q + 1) * P, :], out_sb[:])
+            if unit[1] == CHUNKS - 1:
+                leave_psum3(unit[0])

@@ -20,7 +20,7 @@ CHUNKS = H2 // CHUNK
 CHUNK_BLOCKS = CHUNK // P
 W2_PIECES = 4
 W2_PIECE_CHUNKS = CHUNKS // W2_PIECES
-LEAD = 3
+LEAD = 4
 
 FLOPS = 2 * (D * H1 * N + H1 * H2 * B + H2 * NC * B)
 

@@ -83,24 +83,16 @@ def tile_ternarycreditrisknet_b_kernel(
             nc.tensor.transpose(words_ps[:], table_rows[:, a, :], identity_bf16[:])
             nc.vector.tensor_copy(window[:, a * P : (a + 1) * P], words_ps[:])
 
+        unused = work.tile([P, 1], F32, name="unused")
+        nc.scalar.activation(unused[:], minus_half[:], ACT.Gelu)
+        y1 = [held.tile([P, 2, B], F32, name=f"y1_{g}") for g in range(H1_BLOCKS // 2)]
+        square1 = [held.tile([P, B], F32, name=f"square1_{a}") for a in range(H1_BLOCKS)]
         sum_y1 = held.tile([P, B], F32, name="sum_y1")
         sum_sq1 = held.tile([P, B], F32, name="sum_sq1")
         for sums in (sum_y1, sum_sq1):
             nc.vector.memset(sums[:], 0.0)
-
-        unused = work.tile([P, 1], F32, name="unused")
-        nc.scalar.activation(unused[:], sum_y1[:, 0:1], ACT.Abs_reciprocal_sqrt, bias=1.0, scale=0.0)
-        y1 = [held.tile([P, 2, B], F32, name=f"y1_{g}") for g in range(H1_BLOCKS // 2)]
+        summed_on_vector = [H1_BLOCKS - 1, H1_BLOCKS]
         prod1 = [banks.tile([P, B], F32, name=f"prod1_{a}", tag="bank") for a in range(H1_BLOCKS)]
-
-        def leave_psum1(a, half):
-            records = slice(half * P, (half + 1) * P)
-            y1_block = y1[a // 2][:, a % 2, records]
-            nc.scalar.activation(y1_block, prod1[a][:, records], ACT.Identity, bias=b1_sb[:, a : a + 1], scale=QS / T)
-            square1 = work.tile([P, P], F32, name="square1")
-            nc.scalar.activation(square1[:], prod1[a][:, records], ACT.Square, bias=b1_sb[:, a : a + 1], scale=QS / T)
-            nc.vector.tensor_tensor(sum_y1[:, records], sum_y1[:, records], y1_block, ALU.add)
-            nc.vector.tensor_tensor(sum_sq1[:, records], sum_sq1[:, records], square1[:], ALU.add)
 
         for a in range(H1_BLOCKS):
             for t in range(T):
@@ -111,36 +103,65 @@ def tile_ternarycreditrisknet_b_kernel(
                     start=(t == 0),
                     stop=(t == T - 1),
                 )
-            leave_psum1(a, 0)
 
-        h1 = [held.tile([P, B], BF16, name=f"h1_{a}") for a in range(H1_BLOCKS)]
-        for half in range(HALVES):
+        def leave_psum1(half):
             records = slice(half * P, (half + 1) * P)
-            if half > 0:
-                for a in range(H1_BLOCKS):
-                    leave_psum1(a, half)
-            mean1 = banks.tile([P, P], F32, name="mean1", tag="bank")
-            nc.tensor.matmul(mean1[:], mean_of_h1[:], sum_y1[:, records], start=True, stop=True)
-            mean_sq1 = banks.tile([P, P], F32, name="mean_sq1", tag="bank")
-            nc.tensor.matmul(mean_sq1[:], mean_of_h1[:], sum_sq1[:, records], start=True, stop=True)
-            square_of_mean1 = work.tile([P, P], F32, name="square_of_mean1")
-            nc.scalar.activation(square_of_mean1[:], mean1[:], ACT.Square)
-            var_eps1 = work.tile([P, P], F32, name="var_eps1")
-            nc.vector.scalar_tensor_tensor(
-                var_eps1[:], mean_sq1[:], EPS, square_of_mean1[:], op0=ALU.add, op1=ALU.subtract
-            )
-            rstd1 = work.tile([P, P], F32, name="rstd1")
-            nc.scalar.activation(rstd1[:], var_eps1[:], ACT.Abs_reciprocal_sqrt)
+            for a in range(H1_BLOCKS):
+                bias = b1_sb[:, a : a + 1]
+                y1_block, square_block = y1[a // 2][:, a % 2, records], square1[a][:, records]
+                nc.scalar.activation(y1_block, prod1[a][:, records], ACT.Identity, bias=bias, scale=QS / T)
+                nc.scalar.activation(square_block, prod1[a][:, records], ACT.Square, bias=bias, scale=QS / T)
+                if a < summed_on_vector[half]:
+                    nc.vector.tensor_tensor(sum_y1[:, records], sum_y1[:, records], y1_block, ALU.add)
+                    nc.vector.tensor_tensor(sum_sq1[:, records], sum_sq1[:, records], square_block, ALU.add)
 
-            for g in range(H1_BLOCKS // 2):
-                nc.vector.tensor_tensor(
-                    y1[g][:, :, records], y1[g][:, :, records],
-                    mean1[:].unsqueeze(1).to_broadcast([P, 2, P]), ALU.subtract,
+        def rstd_of_records1(half):
+            records = slice(half * P, (half + 1) * P)
+            mean_column = banks.tile([P, 1], F32, name="mean_column", tag="bank")
+            mean_sq_column = banks.tile([P, 1], F32, name="mean_sq_column", tag="bank")
+            y1_parts, square_parts = [sum_y1[:, records]], [sum_sq1[:, records]]
+            for a in range(summed_on_vector[half], H1_BLOCKS):
+                y1_parts.append(y1[a // 2][:, a % 2, records])
+                square_parts.append(square1[a][:, records])
+            for i in range(len(y1_parts)):
+                for column, parts in ((mean_column, y1_parts), (mean_sq_column, square_parts)):
+                    nc.tensor.matmul(
+                        column[:], parts[i], mean_of_h1[:, 0:1], start=(i == 0), stop=(i == len(parts) - 1)
+                    )
+            sq_less_eps = work.tile([P, 1], F32, name="sq_less_eps")
+            nc.vector.tensor_scalar(
+                sq_less_eps[:], mean_column[:], mean_column[:], EPS, op0=ALU.mult, op1=ALU.subtract
+            )
+            var_eps = work.tile([P, 1], F32, name="var_eps1")
+            nc.vector.tensor_scalar(
+                var_eps[:], mean_sq_column[:], sq_less_eps[:], EPS, op0=ALU.subtract, op1=ALU.max
+            )
+            rstd_column = work.tile([P, 1], F32, name="rstd_column")
+            nc.gpsimd.tensor_tensor(rstd_column[:], var_eps[:], minus_half[:], ALU.pow)
+            return rstd_column
+
+        def subtract_mean1(half):
+            records = slice(half * P, (half + 1) * P)
+            mean_row = banks.tile([P, P], F32, name="mean_row", tag="bank")
+            for a in range(H1_BLOCKS):
+                nc.tensor.matmul(
+                    mean_row[:], mean_of_h1[:], y1[a // 2][:, a % 2, records],
+                    start=(a == 0), stop=(a == H1_BLOCKS - 1),
                 )
             for g in range(H1_BLOCKS // 2):
                 nc.vector.tensor_tensor(
                     y1[g][:, :, records], y1[g][:, :, records],
-                    rstd1[:].unsqueeze(1).to_broadcast([P, 2, P]), ALU.mult,
+                    mean_row[:].unsqueeze(1).to_broadcast([P, 2, P]), ALU.subtract,
+                )
+
+        def norm_gelu1(half, rstd_column):
+            records = slice(half * P, (half + 1) * P)
+            rstd_row = banks.tile([P, P], F32, name="rstd_row", tag="bank")
+            nc.tensor.transpose(rstd_row[:], rstd_column[:].to_broadcast([P, P]), identity_f32[:])
+            for g in range(H1_BLOCKS // 2):
+                nc.vector.tensor_tensor(
+                    y1[g][:, :, records], y1[g][:, :, records],
+                    rstd_row[:].unsqueeze(1).to_broadcast([P, 2, P]), ALU.mult,
                 )
                 for i in range(2):
                     a = 2 * g + i
@@ -148,6 +169,15 @@ def tile_ternarycreditrisknet_b_kernel(
                         h1[a][:, records], y1[g][:, i, records], ACT.Gelu,
                         bias=shift1_sb[:, a : a + 1], scale=gain1_sb[:, a : a + 1],
                     )
+
+        h1 = [held.tile([P, B], BF16, name=f"h1_{a}") for a in range(H1_BLOCKS)]
+        leave_psum1(0)
+        leave_psum1(1)
+        rstd1_of_half0 = rstd_of_records1(0)
+        subtract_mean1(0)
+        rstd1_of_half1 = rstd_of_records1(1)
+        norm_gelu1(0, rstd1_of_half0)
+        subtract_mean1(1)
 
         y2 = [[held.tile([P, CHUNK], F32, name=f"y2_{half}_{c}") for c in range(CHUNKS)] for half in range(HALVES)]
         h2 = [[held.tile([P, P], BF16, name=f"h2_{half}_{a}") for a in range(H2_BLOCKS)] for half in range(HALVES)]
@@ -229,6 +259,8 @@ def tile_ternarycreditrisknet_b_kernel(
 
         units = [(half, c) for half in range(HALVES) for c in range(CHUNKS)]
         for c in range(CHUNKS):
+            if c == 2:
+                norm_gelu1(1, rstd1_of_half1)
             layer2(0, c)
         statistics(0)
         for c in range(CHUNKS):

@@ -18,9 +18,11 @@ HALVES = B // P
 CHUNK = 512
 CHUNKS = H2 // CHUNK
 CHUNK_BLOCKS = CHUNK // P
-W2_PIECES = 4
+W2_PIECES = 2
+PIECE = H2 // W2_PIECES
 W2_PIECE_CHUNKS = CHUNKS // W2_PIECES
-LEAD = 4
+AHEAD = 4
+LEAD = 3
 
 FLOPS = 2 * (D * H1 * N + H1 * H2 * B + H2 * NC * B)
 
@@ -41,26 +43,28 @@ def tile_ternarycreditrisknet_b_kernel(
         w1_sb = held.tile([D, H1], BF16, name="w1_sb")
         nc.sync.dma_start(w1_sb[:], w1)
 
-        def load_columns(vector, name):
-            columns = held.tile([P, vector.shape[0] // P], F32, name=name)
-            nc.sync.dma_start(columns[:], vector.rearrange("(a p) o -> p (a o)", p=P))
-            return columns
-
-        b1_sb = load_columns(b1, "b1_sb")
-        gain1_sb = load_columns(gain1, "gain1_sb")
-        shift1_sb = load_columns(shift1, "shift1_sb")
+        b1_sb = held.tile([P, H1_BLOCKS], F32, name="b1_sb")
+        nc.sync.dma_start(b1_sb[:], b1.rearrange("(a p) o -> p (a o)", p=P))
+        stacked = held.tile([P, P], F32, name="stacked")
+        nc.vector.memset(stacked[:], 0.0)
+        column_of, row = {}, 0
+        for name, vector in (("gain1", gain1), ("shift1", shift1), ("gain2", gain2), ("shift2", shift2), ("b3", b3)):
+            blocks = vector.shape[0] // P
+            nc.sync.dma_start(stacked[row : row + blocks, :], vector.rearrange("(a p) o -> a (p o)", p=P))
+            column_of[name], row = row, row + blocks
 
         w2_view = w2.rearrange("(k p) u -> p k u", p=P)
         w2_pieces = []
         for i in range(W2_PIECES):
-            piece = held.tile([P, H1_BLOCKS, H2 // W2_PIECES], BF16, name=f"w2_piece{i}")
-            nc.sync.dma_start(piece[:], w2_view[:, :, i * (H2 // W2_PIECES) : (i + 1) * (H2 // W2_PIECES)])
-            w2_pieces.append(piece)
-        b2_row = held.tile([P, H2], F32, name="b2_row")
-        nc.sync.dma_start(b2_row[:], b2.rearrange("u o -> (u o)").partition_broadcast(P))
-        gain2_sb = load_columns(gain2, "gain2_sb")
-        shift2_sb = load_columns(shift2, "shift2_sb")
-        b3_sb = load_columns(b3, "b3_sb")
+            w2_piece = held.tile([P, H1_BLOCKS, PIECE], BF16, name=f"w2_piece{i}")
+            nc.sync.dma_start(w2_piece[:], w2_view[:, :, i * PIECE : (i + 1) * PIECE])
+            w2_pieces.append(w2_piece)
+        b2_view = b2.rearrange("u o -> (u o)")
+        b2_pieces = []
+        for i in range(W2_PIECES):
+            b2_piece = held.tile([P, PIECE], F32, name=f"b2_piece{i}")
+            nc.sync.dma_start(b2_piece[:], b2_view[i * PIECE : (i + 1) * PIECE].partition_broadcast(P))
+            b2_pieces.append(b2_piece)
         w3_view = w3.rearrange("(a p) q -> p a q", p=P)
         w3_chunks = []
         for c in range(CHUNKS):
@@ -74,6 +78,9 @@ def tile_ternarycreditrisknet_b_kernel(
         make_identity(nc, identity_f32[:])
         mean_of_h1 = held.tile([P, P], F32, name="mean_of_h1")
         nc.vector.memset(mean_of_h1[:], 1.0 / H1)
+        plus_minus = held.tile([P, 2], F32, name="plus_minus")
+        nc.vector.memset(plus_minus[:, 0:1], 1.0 / H1)
+        nc.vector.memset(plus_minus[:, 1:2], -1.0 / H1)
         minus_half = held.tile([P, 1], F32, name="minus_half")
         nc.vector.memset(minus_half[:], -0.5)
 
@@ -84,7 +91,7 @@ def tile_ternarycreditrisknet_b_kernel(
             nc.vector.tensor_copy(window[:, a * P : (a + 1) * P], words_ps[:])
 
         unused = work.tile([P, 1], F32, name="unused")
-        nc.scalar.activation(unused[:], minus_half[:], ACT.Gelu)
+        nc.scalar.activation(unused[:], mean_of_h1[:, 0:1], ACT.Abs_reciprocal_sqrt)
         y1 = [held.tile([P, 2, B], F32, name=f"y1_{g}") for g in range(H1_BLOCKS // 2)]
         square1 = [held.tile([P, B], F32, name=f"square1_{a}") for a in range(H1_BLOCKS)]
         sum_y1 = held.tile([P, B], F32, name="sum_y1")
@@ -104,6 +111,14 @@ def tile_ternarycreditrisknet_b_kernel(
                     stop=(t == T - 1),
                 )
 
+        columns_ps = banks.tile([P, P], F32, name="columns_ps", tag="bank")
+        nc.tensor.transpose(columns_ps[:], stacked[:], identity_f32[:])
+        columns = held.tile([P, P], F32, name="columns")
+        nc.vector.tensor_copy(columns[:], columns_ps[:])
+
+        def column(name, a):
+            return columns[:, column_of[name] + a : column_of[name] + a + 1]
+
         def leave_psum1(half):
             records = slice(half * P, (half + 1) * P)
             for a in range(H1_BLOCKS):
@@ -115,39 +130,48 @@ def tile_ternarycreditrisknet_b_kernel(
                     nc.vector.tensor_tensor(sum_y1[:, records], sum_y1[:, records], y1_block, ALU.add)
                     nc.vector.tensor_tensor(sum_sq1[:, records], sum_sq1[:, records], square_block, ALU.add)
 
-        def rstd_of_records1(half):
+        def parts_of_y1(half):
             records = slice(half * P, (half + 1) * P)
-            mean_column = banks.tile([P, 1], F32, name="mean_column", tag="bank")
+            blocks = range(summed_on_vector[half], H1_BLOCKS)
+            return [sum_y1[:, records]] + [y1[a // 2][:, a % 2, records] for a in blocks]
+
+        def parts_of_square1(half):
+            records = slice(half * P, (half + 1) * P)
+            return [sum_sq1[:, records]] + [square1[a][:, records] for a in range(summed_on_vector[half], H1_BLOCKS)]
+
+        def rstd_of_records1(half):
+            mean_columns = banks.tile([P, 2], F32, name="mean_columns", tag="bank")
             mean_sq_column = banks.tile([P, 1], F32, name="mean_sq_column", tag="bank")
-            y1_parts, square_parts = [sum_y1[:, records]], [sum_sq1[:, records]]
-            for a in range(summed_on_vector[half], H1_BLOCKS):
-                y1_parts.append(y1[a // 2][:, a % 2, records])
-                square_parts.append(square1[a][:, records])
+            y1_parts, square_parts = parts_of_y1(half), parts_of_square1(half)
+            last = len(y1_parts) - 1
             for i in range(len(y1_parts)):
-                for column, parts in ((mean_column, y1_parts), (mean_sq_column, square_parts)):
-                    nc.tensor.matmul(
-                        column[:], parts[i], mean_of_h1[:, 0:1], start=(i == 0), stop=(i == len(parts) - 1)
-                    )
-            sq_less_eps = work.tile([P, 1], F32, name="sq_less_eps")
+                nc.tensor.matmul(mean_columns[:], y1_parts[i], plus_minus[:], start=(i == 0), stop=(i == last))
+                nc.tensor.matmul(
+                    mean_sq_column[:], square_parts[i], plus_minus[:, 0:1], start=(i == 0), stop=(i == last)
+                )
+            eps_less_sq = work.tile([P, 1], F32, name="eps_less_sq")
             nc.vector.tensor_scalar(
-                sq_less_eps[:], mean_column[:], mean_column[:], EPS, op0=ALU.mult, op1=ALU.subtract
-            )
-            var_eps = work.tile([P, 1], F32, name="var_eps1")
-            nc.vector.tensor_scalar(
-                var_eps[:], mean_sq_column[:], sq_less_eps[:], EPS, op0=ALU.subtract, op1=ALU.max
+                eps_less_sq[:], mean_columns[:, 0:1], mean_columns[:, 1:2], EPS, op0=ALU.mult, op1=ALU.add
             )
             rstd_column = work.tile([P, 1], F32, name="rstd_column")
-            nc.gpsimd.tensor_tensor(rstd_column[:], var_eps[:], minus_half[:], ALU.pow)
+            if half == 0:
+                nc.scalar.activation(
+                    rstd_column[:], mean_sq_column[:], ACT.Abs_reciprocal_sqrt, bias=eps_less_sq[:]
+                )
+            else:
+                var_eps = work.tile([P, 1], F32, name="var_eps1")
+                nc.vector.tensor_scalar(
+                    var_eps[:], mean_sq_column[:], eps_less_sq[:], EPS, op0=ALU.add, op1=ALU.max
+                )
+                nc.gpsimd.tensor_tensor(rstd_column[:], var_eps[:], minus_half[:], ALU.pow)
             return rstd_column
 
         def subtract_mean1(half):
             records = slice(half * P, (half + 1) * P)
             mean_row = banks.tile([P, P], F32, name="mean_row", tag="bank")
-            for a in range(H1_BLOCKS):
-                nc.tensor.matmul(
-                    mean_row[:], mean_of_h1[:], y1[a // 2][:, a % 2, records],
-                    start=(a == 0), stop=(a == H1_BLOCKS - 1),
-                )
+            parts = parts_of_y1(half)
+            for i, part in enumerate(parts):
+                nc.tensor.matmul(mean_row[:], mean_of_h1[:], part, start=(i == 0), stop=(i == len(parts) - 1))
             for g in range(H1_BLOCKS // 2):
                 nc.vector.tensor_tensor(
                     y1[g][:, :, records], y1[g][:, :, records],
@@ -167,7 +191,7 @@ def tile_ternarycreditrisknet_b_kernel(
                     a = 2 * g + i
                     nc.scalar.activation(
                         h1[a][:, records], y1[g][:, i, records], ACT.Gelu,
-                        bias=shift1_sb[:, a : a + 1], scale=gain1_sb[:, a : a + 1],
+                        bias=column("shift1", a), scale=column("gain1", a),
                     )
 
         h1 = [held.tile([P, B], BF16, name=f"h1_{a}") for a in range(H1_BLOCKS)]
@@ -187,16 +211,20 @@ def tile_ternarycreditrisknet_b_kernel(
         rstd2 = [held.tile([P, 1], F32, name=f"rstd2_{half}") for half in range(HALVES)]
         out_ps = [banks.tile([P, B], F32, name=f"out_ps{q}", tag="bank") for q in range(NC_BLOCKS)]
 
-        def layer2(half, c):
-            piece, i = w2_pieces[c // W2_PIECE_CHUNKS], c % W2_PIECE_CHUNKS
+        def product2(half, c):
+            w2_piece, i = w2_pieces[c // W2_PIECE_CHUNKS], c % W2_PIECE_CHUNKS
             prod2 = banks.tile([P, CHUNK], F32, name="prod2", tag="bank")
             for k in range(H1_BLOCKS):
                 nc.tensor.matmul(
-                    prod2[:], h1[k][:, half * P : (half + 1) * P], piece[:, k, i * CHUNK : (i + 1) * CHUNK],
+                    prod2[:], h1[k][:, half * P : (half + 1) * P], w2_piece[:, k, i * CHUNK : (i + 1) * CHUNK],
                     start=(k == 0), stop=(k == H1_BLOCKS - 1),
                 )
+            return prod2
+
+        def leave_psum2(half, c, prod2):
+            b2_piece, i = b2_pieces[c // W2_PIECE_CHUNKS], c % W2_PIECE_CHUNKS
             nc.vector.scalar_tensor_tensor(
-                y2[half][c][:], prod2[:], QS, b2_row[:, c * CHUNK : (c + 1) * CHUNK],
+                y2[half][c][:], prod2[:], QS, b2_piece[:, i * CHUNK : (i + 1) * CHUNK],
                 op0=ALU.mult, op1=ALU.add, accum_out=sums[half][:, c : c + 1],
             )
             squares = work.tile([P, CHUNK], BF16, name="squares")
@@ -230,7 +258,7 @@ def tile_ternarycreditrisknet_b_kernel(
                 a = c * CHUNK_BLOCKS + j
                 nc.scalar.activation(
                     h2[half][a][:], flipped[:, j, :], ACT.Gelu,
-                    bias=shift2_sb[:, a : a + 1], scale=gain2_sb[:, a : a + 1],
+                    bias=column("shift2", a), scale=column("gain2", a),
                 )
 
         def layer3(half, c):
@@ -248,25 +276,27 @@ def tile_ternarycreditrisknet_b_kernel(
                 out_sb = work.tile([P, P], F32, name="out_sb")
                 if q % 2 == 0:
                     nc.scalar.activation(
-                        out_sb[:], out_ps[q][:, records], ACT.Identity, bias=b3_sb[:, q : q + 1], scale=QS
+                        out_sb[:], out_ps[q][:, records], ACT.Identity, bias=column("b3", q), scale=QS
                     )
                     nc.sync.dma_start(out[q * P : (q + 1) * P, records], out_sb[:])
                 else:
                     nc.vector.tensor_scalar(
-                        out_sb[:], out_ps[q][:, records], QS, b3_sb[:, q : q + 1], op0=ALU.mult, op1=ALU.add
+                        out_sb[:], out_ps[q][:, records], QS, column("b3", q), op0=ALU.mult, op1=ALU.add
                     )
                     nc.scalar.dma_start(out[q * P : (q + 1) * P, records], out_sb[:])
 
         units = [(half, c) for half in range(HALVES) for c in range(CHUNKS)]
+        products = [product2(0, c) for c in range(AHEAD)]
+        norm_gelu1(1, rstd1_of_half1)
         for c in range(CHUNKS):
-            if c == 2:
-                norm_gelu1(1, rstd1_of_half1)
-            layer2(0, c)
+            leave_psum2(0, c, products[c])
+            if c + AHEAD < CHUNKS:
+                products.append(product2(0, c + AHEAD))
         statistics(0)
         for c in range(CHUNKS):
             if c >= CHUNKS - LEAD:
                 norm_gelu(*units[c - (CHUNKS - LEAD)])
-            layer2(1, c)
+            leave_psum2(1, c, product2(1, c))
         statistics(1)
         for i, unit in enumerate(units):
             if i + LEAD < len(units):

@@ -1,3 +1,5 @@
+import math
+
 import concourse.mybir as mybir
 from concourse.masks import make_identity
 
@@ -18,8 +20,9 @@ HALVES = B // P
 CHUNK = 512
 CHUNKS = H2 // CHUNK
 CHUNK_BLOCKS = CHUNK // P
-W2_PIECES = 2
+W2_PIECES = 4
 PIECE = H2 // W2_PIECES
+FLIPPED_CHUNKS = CHUNKS // 2
 W2_PIECE_CHUNKS = CHUNKS // W2_PIECES
 AHEAD = 4
 LEAD = 3
@@ -48,7 +51,9 @@ def tile_ternarycreditrisknet_b_kernel(
         stacked = held.tile([P, P], F32, name="stacked")
         nc.vector.memset(stacked[:], 0.0)
         column_of, row = {}, 0
-        for name, vector in (("gain1", gain1), ("shift1", shift1), ("gain2", gain2), ("shift2", shift2), ("b3", b3)):
+        for name, vector in (
+            ("gain1", gain1), ("shift1", shift1), ("b2", b2[: FLIPPED_CHUNKS * CHUNK]), ("gain2", gain2), ("shift2", shift2), ("b3", b3)
+        ):
             blocks = vector.shape[0] // P
             nc.sync.dma_start(stacked[row : row + blocks, :], vector.rearrange("(a p) o -> a (p o)", p=P))
             column_of[name], row = row, row + blocks
@@ -59,12 +64,8 @@ def tile_ternarycreditrisknet_b_kernel(
             w2_piece = held.tile([P, H1_BLOCKS, PIECE], BF16, name=f"w2_piece{i}")
             nc.sync.dma_start(w2_piece[:], w2_view[:, :, i * PIECE : (i + 1) * PIECE])
             w2_pieces.append(w2_piece)
-        b2_view = b2.rearrange("u o -> (u o)")
-        b2_pieces = []
-        for i in range(W2_PIECES):
-            b2_piece = held.tile([P, PIECE], F32, name=f"b2_piece{i}")
-            nc.sync.dma_start(b2_piece[:], b2_view[i * PIECE : (i + 1) * PIECE].partition_broadcast(P))
-            b2_pieces.append(b2_piece)
+        b2_rows = [held.tile([P, FLIPPED_CHUNKS * CHUNK], F32, name="b2_made"), held.tile([P, H2 - FLIPPED_CHUNKS * CHUNK], F32, name="b2_loaded")]
+        nc.sync.dma_start(b2_rows[1][:], b2.rearrange("u o -> (u o)")[FLIPPED_CHUNKS * CHUNK :].partition_broadcast(P))
         w3_view = w3.rearrange("(a p) q -> p a q", p=P)
         w3_chunks = []
         for c in range(CHUNKS):
@@ -194,6 +195,17 @@ def tile_ternarycreditrisknet_b_kernel(
                         bias=column("shift1", a), scale=column("gain1", a),
                     )
 
+        def spread_b2(c):
+            row_ps = banks.tile([P, CHUNK], F32, name="row_ps", tag="bank")
+            for j in range(CHUNK_BLOCKS):
+                b2_column = column("b2", c * CHUNK_BLOCKS + j)
+                nc.tensor.transpose(row_ps[:, j * P : (j + 1) * P], b2_column.to_broadcast([P, P]), identity_f32[:])
+            b2_chunk = b2_rows[0][:, c * CHUNK : (c + 1) * CHUNK]
+            if c % 2 == 0:
+                nc.scalar.copy(b2_chunk, row_ps[:])
+            else:
+                nc.vector.tensor_copy(b2_chunk, row_ps[:])
+
         h1 = [held.tile([P, B], BF16, name=f"h1_{a}") for a in range(H1_BLOCKS)]
         leave_psum1(0)
         leave_psum1(1)
@@ -202,11 +214,13 @@ def tile_ternarycreditrisknet_b_kernel(
         rstd1_of_half1 = rstd_of_records1(1)
         norm_gelu1(0, rstd1_of_half0)
         subtract_mean1(1)
+        for c in range(FLIPPED_CHUNKS):
+            spread_b2(c)
 
         y2 = [[held.tile([P, CHUNK], F32, name=f"y2_{half}_{c}") for c in range(CHUNKS)] for half in range(HALVES)]
         h2 = [[held.tile([P, P], BF16, name=f"h2_{half}_{a}") for a in range(H2_BLOCKS)] for half in range(HALVES)]
         sums = [held.tile([P, CHUNKS], F32, name=f"sums{half}") for half in range(HALVES)]
-        sq_sums = [held.tile([P, CHUNKS], F32, name=f"sq_sums{half}") for half in range(HALVES)]
+        mean_sqs = [held.tile([P, CHUNKS], F32, name=f"mean_sqs{half}") for half in range(HALVES)]
         neg_mean = [held.tile([P, 1], F32, name=f"neg_mean{half}") for half in range(HALVES)]
         rstd2 = [held.tile([P, 1], F32, name=f"rstd2_{half}") for half in range(HALVES)]
         out_ps = [banks.tile([P, B], F32, name=f"out_ps{q}", tag="bank") for q in range(NC_BLOCKS)]
@@ -222,28 +236,28 @@ def tile_ternarycreditrisknet_b_kernel(
             return prod2
 
         def leave_psum2(half, c, prod2):
-            b2_piece, i = b2_pieces[c // W2_PIECE_CHUNKS], c % W2_PIECE_CHUNKS
+            b2_row, i = (b2_rows[0], c) if c < FLIPPED_CHUNKS else (b2_rows[1], c - FLIPPED_CHUNKS)
             nc.vector.scalar_tensor_tensor(
-                y2[half][c][:], prod2[:], QS, b2_piece[:, i * CHUNK : (i + 1) * CHUNK],
+                y2[half][c][:], prod2[:], QS, b2_row[:, i * CHUNK : (i + 1) * CHUNK],
                 op0=ALU.mult, op1=ALU.add, accum_out=sums[half][:, c : c + 1],
             )
             squares = work.tile([P, CHUNK], BF16, name="squares")
-            nc.scalar.activation(squares[:], y2[half][c][:], ACT.Square, accum_out=sq_sums[half][:, c : c + 1])
+            nc.scalar.activation(
+                squares[:], y2[half][c][:], ACT.Square, scale=1.0 / math.sqrt(H2), accum_out=mean_sqs[half][:, c : c + 1]
+            )
 
         def statistics(half):
             total = work.tile([P, 1], F32, name="total")
             nc.vector.reduce_sum(total[:], sums[half][:], axis=ALONG_FREE)
             nc.vector.tensor_scalar_mul(neg_mean[half][:], total[:], -1.0 / H2)
-            total_sq = work.tile([P, 1], F32, name="total_sq")
-            nc.vector.reduce_sum(total_sq[:], sq_sums[half][:], axis=ALONG_FREE)
-            square_of_mean = work.tile([P, 1], F32, name="square_of_mean")
-            nc.vector.tensor_tensor(square_of_mean[:], neg_mean[half][:], neg_mean[half][:], ALU.mult)
-            var = work.tile([P, 1], F32, name="var")
-            nc.vector.scalar_tensor_tensor(
-                var[:], total_sq[:], 1.0 / H2, square_of_mean[:], op0=ALU.mult, op1=ALU.subtract
+            sq_less_eps = work.tile([P, 1], F32, name="sq_less_eps")
+            nc.vector.tensor_scalar(
+                sq_less_eps[:], neg_mean[half][:], neg_mean[half][:], EPS, op0=ALU.mult, op1=ALU.subtract
             )
+            mean_sq = work.tile([P, 1], F32, name="mean_sq")
+            nc.vector.reduce_sum(mean_sq[:], mean_sqs[half][:], axis=ALONG_FREE)
             var_eps = work.tile([P, 1], F32, name="var_eps")
-            nc.vector.tensor_scalar(var_eps[:], var[:], 0.0, EPS, op0=ALU.max, op1=ALU.add)
+            nc.vector.tensor_scalar(var_eps[:], mean_sq[:], sq_less_eps[:], EPS, op0=ALU.subtract, op1=ALU.max)
             nc.gpsimd.tensor_tensor(rstd2[half][:], var_eps[:], minus_half[:], ALU.pow)
 
         def norm_gelu(half, c):

import math

import concourse.mybir as mybir
from concourse.masks import make_identity

BF16, F32, U16 = mybir.dt.bfloat16, mybir.dt.float32, mybir.dt.uint16
ACT = mybir.ActivationFunctionType
ALU = mybir.AluOpType
ALONG_FREE = mybir.AxisListType.X

P = 128
V, D, H1, H2, NC = 512, 128, 512, 4096, 512
T, B = 4, 256
N = T * B
QS = 0.5
EPS = 1e-5

H1_BLOCKS, H2_BLOCKS, NC_BLOCKS = H1 // P, H2 // P, NC // P
HALVES = B // P
CHUNK = 512
CHUNKS = H2 // CHUNK
CHUNK_BLOCKS = CHUNK // P
W2_PIECES = 4
PIECE = H2 // W2_PIECES
FLIPPED_CHUNKS = CHUNKS // 2
W2_PIECE_CHUNKS = CHUNKS // W2_PIECES
AHEAD = 4
LEAD = 3

FLOPS = 2 * (D * H1 * N + H1 * H2 * B + H2 * NC * B)


def tile_ternarycreditrisknet_b_kernel(
    tc, table, w1, b1, gain1, shift1, w2, b2, gain2, shift2, w3, b3, offs, out
):
    nc = tc.nc
    with (
        tc.tile_pool(name="held", bufs=1) as held,
        tc.tile_pool(name="work", bufs=4) as work,
        tc.psum_pool(name="banks", bufs=8) as banks,
    ):
        table_rows = held.tile([P, V // P, D], BF16, name="table_rows")
        nc.sync.dma_start(table_rows[:], table.rearrange("(a p) d -> p a d", p=P))
        offsets = held.tile([P, N // 16], U16, name="offsets")
        nc.sync.dma_start(offsets[:], offs)
        w1_sb = held.tile([D, H1], BF16, name="w1_sb")
        nc.sync.dma_start(w1_sb[:], w1)

        b1_sb = held.tile([P, H1_BLOCKS], F32, name="b1_sb")
        nc.sync.dma_start(b1_sb[:], b1.rearrange("(a p) o -> p (a o)", p=P))
        stacked = held.tile([P, P], F32, name="stacked")
        nc.vector.memset(stacked[:], 0.0)
        column_of, row = {}, 0
        for name, vector in (
            ("gain1", gain1), ("shift1", shift1), ("b2", b2[: FLIPPED_CHUNKS * CHUNK]), ("gain2", gain2), ("shift2", shift2), ("b3", b3)
        ):
            blocks = vector.shape[0] // P
            nc.sync.dma_start(stacked[row : row + blocks, :], vector.rearrange("(a p) o -> a (p o)", p=P))
            column_of[name], row = row, row + blocks

        w2_view = w2.rearrange("(k p) u -> p k u", p=P)
        w2_pieces = []
        for i in range(W2_PIECES):
            w2_piece = held.tile([P, H1_BLOCKS, PIECE], BF16, name=f"w2_piece{i}")
            nc.sync.dma_start(w2_piece[:], w2_view[:, :, i * PIECE : (i + 1) * PIECE])
            w2_pieces.append(w2_piece)
        b2_rows = [held.tile([P, FLIPPED_CHUNKS * CHUNK], F32, name="b2_made"), held.tile([P, H2 - FLIPPED_CHUNKS * CHUNK], F32, name="b2_loaded")]
        nc.sync.dma_start(b2_rows[1][:], b2.rearrange("u o -> (u o)")[FLIPPED_CHUNKS * CHUNK :].partition_broadcast(P))
        w3_view = w3.rearrange("(a p) q -> p a q", p=P)
        w3_chunks = []
        for c in range(CHUNKS):
            chunk = held.tile([P, CHUNK_BLOCKS, NC], BF16, name=f"w3_chunk{c}")
            nc.sync.dma_start(chunk[:], w3_view[:, c * CHUNK_BLOCKS : (c + 1) * CHUNK_BLOCKS, :])
            w3_chunks.append(chunk)

        identity_bf16 = held.tile([P, P], BF16, name="identity_bf16")
        make_identity(nc, identity_bf16[:])
        identity_f32 = held.tile([P, P], F32, name="identity_f32")
        make_identity(nc, identity_f32[:])
        mean_of_h1 = held.tile([P, P], F32, name="mean_of_h1")
        nc.vector.memset(mean_of_h1[:], 1.0 / H1)
        plus_minus = held.tile([P, 2], F32, name="plus_minus")
        nc.vector.memset(plus_minus[:, 0:1], 1.0 / H1)
        nc.vector.memset(plus_minus[:, 1:2], -1.0 / H1)
        minus_half = held.tile([P, 1], F32, name="minus_half")
        nc.vector.memset(minus_half[:], -0.5)

        window = held.tile([D, V], BF16, name="window")
        for a in range(V // P):
            words_ps = banks.tile([D, P], BF16, name="words_ps", tag="bank")
            nc.tensor.transpose(words_ps[:], table_rows[:, a, :], identity_bf16[:])
            nc.vector.tensor_copy(window[:, a * P : (a + 1) * P], words_ps[:])

        unused = work.tile([P, 1], F32, name="unused")
        nc.scalar.activation(unused[:], mean_of_h1[:, 0:1], ACT.Abs_reciprocal_sqrt)
        y1 = [held.tile([P, 2, B], F32, name=f"y1_{g}") for g in range(H1_BLOCKS // 2)]
        square1 = [held.tile([P, B], F32, name=f"square1_{a}") for a in range(H1_BLOCKS)]
        sum_y1 = held.tile([P, B], F32, name="sum_y1")
        sum_sq1 = held.tile([P, B], F32, name="sum_sq1")
        for sums in (sum_y1, sum_sq1):
            nc.vector.memset(sums[:], 0.0)
        summed_on_vector = [H1_BLOCKS - 1, H1_BLOCKS]
        prod1 = [banks.tile([P, B], F32, name=f"prod1_{a}", tag="bank") for a in range(H1_BLOCKS)]

        for a in range(H1_BLOCKS):
            for t in range(T):
                nc.tensor.matmul(
                    prod1[a][:],
                    w1_sb[:, a * P : (a + 1) * P],
                    window[:].indirect(offsets[:, t * (B // 16) : (t + 1) * (B // 16)]),
                    start=(t == 0),
                    stop=(t == T - 1),
                )

        columns_ps = banks.tile([P, P], F32, name="columns_ps", tag="bank")
        nc.tensor.transpose(columns_ps[:], stacked[:], identity_f32[:])
        columns = held.tile([P, P], F32, name="columns")
        nc.vector.tensor_copy(columns[:], columns_ps[:])

        def column(name, a):
            return columns[:, column_of[name] + a : column_of[name] + a + 1]

        def leave_psum1(half):
            records = slice(half * P, (half + 1) * P)
            for a in range(H1_BLOCKS):
                bias = b1_sb[:, a : a + 1]
                y1_block, square_block = y1[a // 2][:, a % 2, records], square1[a][:, records]
                nc.scalar.activation(y1_block, prod1[a][:, records], ACT.Identity, bias=bias, scale=QS / T)
                nc.scalar.activation(square_block, prod1[a][:, records], ACT.Square, bias=bias, scale=QS / T)
                if a < summed_on_vector[half]:
                    nc.vector.tensor_tensor(sum_y1[:, records], sum_y1[:, records], y1_block, ALU.add)
                    nc.vector.tensor_tensor(sum_sq1[:, records], sum_sq1[:, records], square_block, ALU.add)

        def parts_of_y1(half):
            records = slice(half * P, (half + 1) * P)
            blocks = range(summed_on_vector[half], H1_BLOCKS)
            return [sum_y1[:, records]] + [y1[a // 2][:, a % 2, records] for a in blocks]

        def parts_of_square1(half):
            records = slice(half * P, (half + 1) * P)
            return [sum_sq1[:, records]] + [square1[a][:, records] for a in range(summed_on_vector[half], H1_BLOCKS)]

        def rstd_of_records1(half):
            mean_columns = banks.tile([P, 2], F32, name="mean_columns", tag="bank")
            mean_sq_column = banks.tile([P, 1], F32, name="mean_sq_column", tag="bank")
            y1_parts, square_parts = parts_of_y1(half), parts_of_square1(half)
            last = len(y1_parts) - 1
            for i in range(len(y1_parts)):
                nc.tensor.matmul(mean_columns[:], y1_parts[i], plus_minus[:], start=(i == 0), stop=(i == last))
                nc.tensor.matmul(
                    mean_sq_column[:], square_parts[i], plus_minus[:, 0:1], start=(i == 0), stop=(i == last)
                )
            eps_less_sq = work.tile([P, 1], F32, name="eps_less_sq")
            nc.vector.tensor_scalar(
                eps_less_sq[:], mean_columns[:, 0:1], mean_columns[:, 1:2], EPS, op0=ALU.mult, op1=ALU.add
            )
            rstd_column = work.tile([P, 1], F32, name="rstd_column")
            if half == 0:
                nc.scalar.activation(
                    rstd_column[:], mean_sq_column[:], ACT.Abs_reciprocal_sqrt, bias=eps_less_sq[:]
                )
            else:
                var_eps = work.tile([P, 1], F32, name="var_eps1")
                nc.vector.tensor_scalar(
                    var_eps[:], mean_sq_column[:], eps_less_sq[:], EPS, op0=ALU.add, op1=ALU.max
                )
                nc.gpsimd.tensor_tensor(rstd_column[:], var_eps[:], minus_half[:], ALU.pow)
            return rstd_column

        def subtract_mean1(half):
            records = slice(half * P, (half + 1) * P)
            mean_row = banks.tile([P, P], F32, name="mean_row", tag="bank")
            parts = parts_of_y1(half)
            for i, part in enumerate(parts):
                nc.tensor.matmul(mean_row[:], mean_of_h1[:], part, start=(i == 0), stop=(i == len(parts) - 1))
            for g in range(H1_BLOCKS // 2):
                nc.vector.tensor_tensor(
                    y1[g][:, :, records], y1[g][:, :, records],
                    mean_row[:].unsqueeze(1).to_broadcast([P, 2, P]), ALU.subtract,
                )

        def norm_gelu1(half, rstd_column):
            records = slice(half * P, (half + 1) * P)
            rstd_row = banks.tile([P, P], F32, name="rstd_row", tag="bank")
            nc.tensor.transpose(rstd_row[:], rstd_column[:].to_broadcast([P, P]), identity_f32[:])
            for g in range(H1_BLOCKS // 2):
                nc.vector.tensor_tensor(
                    y1[g][:, :, records], y1[g][:, :, records],
                    rstd_row[:].unsqueeze(1).to_broadcast([P, 2, P]), ALU.mult,
                )
                for i in range(2):
                    a = 2 * g + i
                    nc.scalar.activation(
                        h1[a][:, records], y1[g][:, i, records], ACT.Gelu,
                        bias=column("shift1", a), scale=column("gain1", a),
                    )

        def spread_b2(c):
            row_ps = banks.tile([P, CHUNK], F32, name="row_ps", tag="bank")
            for j in range(CHUNK_BLOCKS):
                b2_column = column("b2", c * CHUNK_BLOCKS + j)
                nc.tensor.transpose(row_ps[:, j * P : (j + 1) * P], b2_column.to_broadcast([P, P]), identity_f32[:])
            b2_chunk = b2_rows[0][:, c * CHUNK : (c + 1) * CHUNK]
            if c % 2 == 0:
                nc.scalar.copy(b2_chunk, row_ps[:])
            else:
                nc.vector.tensor_copy(b2_chunk, row_ps[:])

        h1 = [held.tile([P, B], BF16, name=f"h1_{a}") for a in range(H1_BLOCKS)]
        leave_psum1(0)
        leave_psum1(1)
        rstd1_of_half0 = rstd_of_records1(0)
        subtract_mean1(0)
        rstd1_of_half1 = rstd_of_records1(1)
        norm_gelu1(0, rstd1_of_half0)
        subtract_mean1(1)
        for c in range(FLIPPED_CHUNKS):
            spread_b2(c)

        y2 = [[held.tile([P, CHUNK], F32, name=f"y2_{half}_{c}") for c in range(CHUNKS)] for half in range(HALVES)]
        h2 = [[held.tile([P, P], BF16, name=f"h2_{half}_{a}") for a in range(H2_BLOCKS)] for half in range(HALVES)]
        sums = [held.tile([P, CHUNKS], F32, name=f"sums{half}") for half in range(HALVES)]
        mean_sqs = [held.tile([P, CHUNKS], F32, name=f"mean_sqs{half}") for half in range(HALVES)]
        neg_mean = [held.tile([P, 1], F32, name=f"neg_mean{half}") for half in range(HALVES)]
        rstd2 = [held.tile([P, 1], F32, name=f"rstd2_{half}") for half in range(HALVES)]
        out_ps = [banks.tile([P, B], F32, name=f"out_ps{q}", tag="bank") for q in range(NC_BLOCKS)]

        def product2(half, c):
            w2_piece, i = w2_pieces[c // W2_PIECE_CHUNKS], c % W2_PIECE_CHUNKS
            prod2 = banks.tile([P, CHUNK], F32, name="prod2", tag="bank")
            for k in range(H1_BLOCKS):
                nc.tensor.matmul(
                    prod2[:], h1[k][:, half * P : (half + 1) * P], w2_piece[:, k, i * CHUNK : (i + 1) * CHUNK],
                    start=(k == 0), stop=(k == H1_BLOCKS - 1),
                )
            return prod2

        def leave_psum2(half, c, prod2):
            b2_row, i = (b2_rows[0], c) if c < FLIPPED_CHUNKS else (b2_rows[1], c - FLIPPED_CHUNKS)
            nc.vector.scalar_tensor_tensor(
                y2[half][c][:], prod2[:], QS, b2_row[:, i * CHUNK : (i + 1) * CHUNK],
                op0=ALU.mult, op1=ALU.add, accum_out=sums[half][:, c : c + 1],
            )
            squares = work.tile([P, CHUNK], BF16, name="squares")
            nc.scalar.activation(
                squares[:], y2[half][c][:], ACT.Square, scale=1.0 / math.sqrt(H2), accum_out=mean_sqs[half][:, c : c + 1]
            )

        def statistics(half):
            total = work.tile([P, 1], F32, name="total")
            nc.vector.reduce_sum(total[:], sums[half][:], axis=ALONG_FREE)
            nc.vector.tensor_scalar_mul(neg_mean[half][:], total[:], -1.0 / H2)
            sq_less_eps = work.tile([P, 1], F32, name="sq_less_eps")
            nc.vector.tensor_scalar(
                sq_less_eps[:], neg_mean[half][:], neg_mean[half][:], EPS, op0=ALU.mult, op1=ALU.subtract
            )
            mean_sq = work.tile([P, 1], F32, name="mean_sq")
            nc.vector.reduce_sum(mean_sq[:], mean_sqs[half][:], axis=ALONG_FREE)
            var_eps = work.tile([P, 1], F32, name="var_eps")
            nc.vector.tensor_scalar(var_eps[:], mean_sq[:], sq_less_eps[:], EPS, op0=ALU.subtract, op1=ALU.max)
            nc.gpsimd.tensor_tensor(rstd2[half][:], var_eps[:], minus_half[:], ALU.pow)

        def norm_gelu(half, c):
            normed = y2[half][c]
            nc.vector.tensor_scalar(
                normed[:], normed[:], neg_mean[half][:], rstd2[half][:], op0=ALU.add, op1=ALU.mult
            )
            flipped = banks.tile([P, CHUNK_BLOCKS, P], F32, name="flipped", tag="bank")
            for j in range(CHUNK_BLOCKS):
                nc.tensor.transpose(flipped[:, j, :], normed[:, j * P : (j + 1) * P], identity_f32[:])
            for j in range(CHUNK_BLOCKS):
                a = c * CHUNK_BLOCKS + j
                nc.scalar.activation(
                    h2[half][a][:], flipped[:, j, :], ACT.Gelu,
                    bias=column("shift2", a), scale=column("gain2", a),
                )

        def layer3(half, c):
            for q in range(NC_BLOCKS):
                for j in range(CHUNK_BLOCKS):
                    a = c * CHUNK_BLOCKS + j
                    nc.tensor.matmul(
                        out_ps[q][:, half * P : (half + 1) * P], w3_chunks[c][:, j, q * P : (q + 1) * P], h2[half][a][:],
                        start=(a == 0), stop=(a == H2_BLOCKS - 1),
                    )

        def leave_psum3(half):
            records = slice(half * P, (half + 1) * P)
            for q in range(NC_BLOCKS):
                out_sb = work.tile([P, P], F32, name="out_sb")
                if q % 2 == 0:
                    nc.scalar.activation(
                        out_sb[:], out_ps[q][:, records], ACT.Identity, bias=column("b3", q), scale=QS
                    )
                    nc.sync.dma_start(out[q * P : (q + 1) * P, records], out_sb[:])
                else:
                    nc.vector.tensor_scalar(
                        out_sb[:], out_ps[q][:, records], QS, column("b3", q), op0=ALU.mult, op1=ALU.add
                    )
                    nc.scalar.dma_start(out[q * P : (q + 1) * P, records], out_sb[:])

        units = [(half, c) for half in range(HALVES) for c in range(CHUNKS)]
        products = [product2(0, c) for c in range(AHEAD)]
        norm_gelu1(1, rstd1_of_half1)
        for c in range(CHUNKS):
            leave_psum2(0, c, products[c])
            if c + AHEAD < CHUNKS:
                products.append(product2(0, c + AHEAD))
        statistics(0)
        for c in range(CHUNKS):
            if c >= CHUNKS - LEAD:
                norm_gelu(*units[c - (CHUNKS - LEAD)])
            leave_psum2(1, c, product2(1, c))
        statistics(1)
        for i, unit in enumerate(units):
            if i + LEAD < len(units):
                norm_gelu(*units[i + LEAD])
            layer3(*unit)
            if unit[1] == CHUNKS - 1:
                leave_psum3(unit[0])
